import numpy as np
import ml_dtypes


def mxq(x, axis, fmt="e4m3"):
    dtype, down = {"e4m3": (ml_dtypes.float8_e4m3fn, 7), "e5m2": (ml_dtypes.float8_e5m2, 14)}[fmt]
    v = np.moveaxis(np.asarray(x, np.float32).astype(ml_dtypes.bfloat16).astype(np.float64), axis, -1)
    blocks = v.reshape(v.shape[:-1] + (-1, 32))
    amax = np.abs(blocks).max(-1, keepdims=True)
    byte = np.maximum(np.where(amax > 0, np.frexp(amax)[1] - 1 + 127, 0) - down, 1)
    scale = np.exp2(byte - 127.0)
    codes = (blocks / scale).astype(np.float32).astype(dtype).astype(np.float64)
    return np.moveaxis((codes * scale).reshape(v.shape), -1, axis)


WIDE = False


def mx_kscale(k):
    if not WIDE:
        return np.ones(k)
    levels = np.array([10, -10, 5, -5, 0])
    if k % 512:
        return np.exp2(np.random.permutation(np.resize(levels, k // 32))).repeat(32)
    a = np.empty((k // 512, 16))
    for p in range(k // 512):
        a[p, :8] = np.random.permutation(np.resize(levels, 8))
        for g in range(8):
            far = levels[np.abs(levels - a[p, g]) >= 10]
            a[p, g + 8] = far[np.random.randint(len(far))]
    return np.exp2(a.ravel()).repeat(32)


BF16 = ml_dtypes.bfloat16


def bf(x):
    return np.asarray(x, np.float32).astype(BF16)


def f64(x):
    return np.asarray(x).astype(np.float64)


B, L, DIM, H, D = 4, 2048, 1024, 2, 64
EPS = 1e-6
THETA = 10000.0


def rope_table(seq_len, head_dim):
    pos = np.arange(seq_len, dtype=np.float64)
    inv = 1.0 / (THETA ** (np.arange(0, head_dim, 2, dtype=np.float64) / head_dim))
    ang = pos[:, None] * inv[None, :]
    cos, sin = np.cos(ang), np.sin(ang)
    rot = np.stack([np.stack([cos, -sin], -1), np.stack([sin, cos], -1)], -2)
    return rot[None, None]


def rms_norm(u, gain):
    rrms = 1.0 / np.sqrt(np.mean(np.square(u), axis=-1, keepdims=True) + EPS)
    return u * rrms * gain


def rope(u, table):
    ur = u.reshape(*u.shape[:-1], -1, 1, 2)
    out = table[..., 0] * ur[..., 0] + table[..., 1] * ur[..., 1]
    return out.reshape(u.shape)


def setup_inputs():
    s = mx_kscale(DIM)
    return {"x": bf(np.random.standard_normal((B, L, DIM)) * s),
            "pe": bf(rope_table(L, D)),
            "qkv_w": bf(np.random.standard_normal((DIM, 3 * H * D)) / np.sqrt(DIM) / s[:, None]),
            "qkv_b": bf(np.random.standard_normal(3 * H * D) * 0.2),
            "q_scale": bf(1.0 + 0.1 * np.random.standard_normal(D)),
            "k_scale": bf(1.0 + 0.1 * np.random.standard_normal(D))}


def reference(x, pe, qkv_w, qkv_b, q_scale, k_scale):
    qkv = (mxq(f64(x), 2, "e4m3") @ mxq(f64(qkv_w), 0, "e4m3")) + f64(qkv_b)
    qkv = qkv.reshape(B, L, 3, H, D).transpose(2, 0, 3, 1, 4)
    q, k, v = qkv[0], qkv[1], qkv[2]
    q = rms_norm(q, f64(q_scale))
    k = rms_norm(k, f64(k_scale))
    table = f64(pe)
    return rope(q, table), rope(k, table), v

@@ -1,0 +1,316 @@
+from contextlib import ExitStack
+
+import concourse.mybir as mybir
+from concourse.masks import make_identity
+
+F32 = mybir.dt.float32
+BF16 = mybir.dt.bfloat16
+U32 = mybir.dt.uint32
+U8 = mybir.dt.uint8
+FP8X4 = mybir.dt.float8_e4m3fn_x4
+ALU = mybir.AluOpType
+ACT = mybir.ActivationFunctionType
+
+B, L, DIM, H, D = 4, 2048, 1024, 2, 64
+EPS = 1e-6
+P = 128
+TPB = L // P
+RT = 4
+RPB = TPB // RT
+ROUNDS = B * RPB
+GROUPS = RT * 2 * H
+QK = 2 * H * D
+PAIRS = D // 2
+WORDS = DIM // 2
+BANK = 512
+NX = 6
+GPSIMD_GROUPS = 11
+GPSIMD_GROUPS_LAST = 5
+FLOPS = 2 * B * L * DIM * 3 * H * D
+
+
+def tile_selfattention_pa_t_kernel(tc, x, pe, qkv_w, qkv_b, q_scale, k_scale, out_0, out_1, out_2):
+    nc = tc.nc
+    with ExitStack() as ctx:
+        const = ctx.enter_context(tc.tile_pool(name="const", bufs=1))
+        xpool = ctx.enter_context(tc.tile_pool(name="xpool", bufs=NX))
+        gpool = ctx.enter_context(tc.tile_pool(name="gpool", bufs=3))
+        cpool = ctx.enter_context(tc.tile_pool(name="cpool", bufs=2))
+        ypool = ctx.enter_context(tc.tile_pool(name="ypool", bufs=2))
+        ppool = ctx.enter_context(tc.tile_pool(name="ppool", bufs=2))
+        spool = ctx.enter_context(tc.tile_pool(name="spool", bufs=2))
+        jpool = ctx.enter_context(tc.tile_pool(name="jpool", bufs=2))
+        small = ctx.enter_context(tc.tile_pool(name="small", bufs=3))
+        stage = ctx.enter_context(tc.tile_pool(name="stage", bufs=2))
+        psum_tp = ctx.enter_context(tc.psum_pool(name="psum_tp", bufs=4))
+        psum_qk = ctx.enter_context(tc.psum_pool(name="psum_qk", bufs=2))
+        psum_v = ctx.enter_context(tc.psum_pool(name="psum_v", bufs=2))
+        ctx.enter_context(tc.manual_schedule())
+
+        xts, tps, groupeds, codes, planes = {}, {}, {}, {}, {}
+        qkbanks, vbanks, ys, prods, sums, rrs, stages = {}, {}, {}, {}, {}, {}, {}
+
+        def load(r):
+            b, j = divmod(r, RPB)
+            xt = xpool.tile([P, RT * DIM], BF16, name="xt", tag="xt")
+            src = x[b].rearrange("(p t) k -> p (t k)", t=TPB)
+            first = j * RT * DIM
+            cuts = 2 if r == 0 else 1
+            width = RT * DIM // cuts
+            for c in range(cuts):
+                nc.sync.dma_start(
+                    out=xt[:, c * width:(c + 1) * width],
+                    in_=src[:, first + c * width:first + (c + 1) * width],
+                )
+            xts[r] = xt
+
+        ident = const.tile([P, P], F32, name="ident", tag="ident")
+        make_identity(nc, ident[:])
+        ones = const.tile([P, P], BF16, name="ones", tag="ones")
+        nc.vector.memset(ones[:], 1.0)
+        row = const.tile([P, BANK], BF16, name="row", tag="row")
+        nc.vector.memset(row[:], 0.0)
+        eps = const.tile([P, 1], F32, name="eps", tag="eps")
+        nc.vector.memset(eps[:], EPS)
+        junk = const.tile([P, D], F32, name="junk", tag="junk")
+
+        w_raw = const.tile([P, 8, 3 * P], BF16, name="w_raw", tag="w_raw")
+        nc.sync.dma_start(
+            out=w_raw[:].rearrange("p (g t) n -> p g (t n)", t=4),
+            in_=qkv_w.rearrange("(g q t) n -> q g (t n)", g=2, t=4),
+        )
+        nc.sync.dma_start(out=row[0:1, 0:3 * P], in_=qkv_b.unsqueeze(0))
+        nc.sync.dma_start(out=row[0:1, 3 * P:3 * P + D], in_=q_scale.unsqueeze(0))
+        nc.sync.dma_start(out=row[0:1, 3 * P + D:BANK], in_=k_scale.unsqueeze(0))
+        load(0)
+        pe_sb = const.tile([P, TPB * 4 * PAIRS], BF16, name="pe_sb", tag="pe_sb")
+        nc.sync.dma_start(out=pe_sb[:], in_=pe[0, 0].rearrange("(p t) i a b -> p (t i a b)", t=TPB))
+        for r in range(1, NX):
+            load(r)
+        nc.scalar.activation(out=junk[:, 0:1], in_=eps[:], func=ACT.Abs_reciprocal_sqrt)
+
+        wg_qk = const.tile([P, 2, QK, 4], BF16, name="wg_qk", tag="wg_qk", align_bytes=64)
+        wg_v = const.tile([P, 2, P, 4], BF16, name="wg_v", tag="wg_v", align_bytes=64)
+        for g in range(2):
+            for b in range(2):
+                nc.vector.tensor_copy(
+                    out=wg_qk[:, g].rearrange("p (n b i) t -> p n b i t", n=4, b=2)[:, :, b],
+                    in_=w_raw[:, 4 * g:4 * g + 4, 0:QK].rearrange("p t (n i b) -> p n i t b", i=PAIRS, b=2)[:, :, :, :, b],
+                )
+            nc.scalar.copy(out=wg_v[:, g], in_=w_raw[:, 4 * g:4 * g + 4, QK:3 * P].rearrange("p t n -> p n t"))
+        wc_qk = const.tile([P, 2 * QK], U32, name="wc_qk", tag="wc_qk", align_bytes=64)
+        ws_qk = const.tile([P, 2 * QK], U8, name="ws_qk", tag="ws_qk", align_bytes=64)
+        wc_v = const.tile([P, 2 * P], U32, name="wc_v", tag="wc_v", align_bytes=64)
+        ws_v = const.tile([P, 2 * P], U8, name="ws_v", tag="ws_v", align_bytes=64)
+        nc.vector.quantize_mx(out=wc_qk[:].bitcast(FP8X4), scales=ws_qk[:], in_=wg_qk[:].rearrange("p g n t -> p (g n t)"))
+        nc.vector.quantize_mx(out=wc_v[:].bitcast(FP8X4), scales=ws_v[:], in_=wg_v[:].rearrange("p g n t -> p (g n t)"))
+
+        cps = psum_v.tile([P, BANK], F32, name="cps", tag="vb")
+        nc.tensor.matmul(out=cps[:], lhsT=ones[:], rhs=row[:], start=True, stop=True)
+        bias_qk = const.tile([P, QK], F32, name="bias_qk", tag="bias_qk")
+        nc.vector.tensor_copy(
+            out=bias_qk[:].rearrange("p (n b i) -> p n b i", b=2, i=PAIRS),
+            in_=cps[:, 0:QK].rearrange("p (n i b) -> p n b i", i=PAIRS, b=2),
+        )
+        cv = const.tile([P, QK], F32, name="cv", tag="cv")
+        nc.vector.tensor_copy(out=cv[:], in_=cps[:, QK:BANK])
+
+        tab = const.tile([P, TPB, 2, 2, D], F32, name="tab", tag="tab")
+
+        def table(s, b):
+            gain = cv[:, P + s * D:P + (s + 1) * D].rearrange("p (i b) -> p b i", b=2)[:, b, :]
+            nc.vector.tensor_tensor(
+                out=tab[:, :, s, b, :].rearrange("p t (a i) -> p t a i", a=2),
+                in0=pe_sb[:].rearrange("p (t i a b) -> p t a i b", i=PAIRS, a=2, b=2)[:, :, :, :, b],
+                in1=gain.unsqueeze(1).unsqueeze(1).to_broadcast([P, TPB, 2, PAIRS]),
+                op=ALU.mult,
+            )
+
+        def transposes(r):
+            words = xts[r][:].bitcast(F32)
+            banks = []
+            for tt in range(RT):
+                tp = psum_tp.tile([P, 4, P], F32, name="tp", tag="tp")
+                for c in range(4):
+                    col = tt * WORDS + (c // 2) * 2 * P + c % 2
+                    nc.tensor.transpose(tp[:, c, :], words[:, col:col + 2 * P - 1:2], ident[:])
+                banks.append(tp)
+            tps[r] = banks
+            if r + NX < ROUNDS:
+                load(r + NX)
+
+        def copy_out(r):
+            grouped = gpool.tile([P, RT * DIM], BF16, name="grouped", tag="grouped", align_bytes=64)
+            gw = grouped[:].bitcast(F32)
+            for tt in range(RT):
+                nc.scalar.copy(
+                    out=gw[:, tt * WORDS:(tt + 1) * WORDS].rearrange("p (g r u) -> p g r u", g=2, u=2),
+                    in_=tps[r][tt][:].rearrange("p (g u) r -> p g r u", u=2),
+                )
+            groupeds[r] = grouped
+
+        def quantise(r, cuts):
+            xc = cpool.tile([P, RT * 2 * P], U32, name="xc", tag="xc", align_bytes=64)
+            xs = cpool.tile([P, RT * 2 * P], U8, name="xs", tag="xs", align_bytes=64)
+            codes[r], planes[r] = xc, xs
+            width = RT * 2 * P // cuts
+
+            def part(c):
+                nc.vector.quantize_mx(
+                    out=xc[:, c * width:(c + 1) * width].bitcast(FP8X4),
+                    scales=xs[:, c * width:(c + 1) * width],
+                    in_=groupeds[r][:, 4 * c * width:4 * (c + 1) * width],
+                )
+
+            return part
+
+        def project(r):
+            xc, xs = codes[r], planes[r]
+            qk = []
+            for half in range(2):
+                qkb = psum_qk.tile([P, BANK], F32, name="qkb", tag="qkb")
+                qk.append(qkb)
+            vb = psum_v.tile([P, BANK], F32, name="vb", tag="vb")
+            for tt in range(RT):
+                for g in range(2):
+                    sl = slice((tt * 2 + g) * P, (tt * 2 + g + 1) * P)
+                    nc.tensor.matmul_mx(
+                        out=qk[tt // 2][:, (tt % 2) * QK:(tt % 2 + 1) * QK],
+                        lhsT=xc[:, sl].bitcast(FP8X4), lhsT_scale=xs[:, sl],
+                        rhs=wc_qk[:, g * QK:(g + 1) * QK].bitcast(FP8X4), rhs_scale=ws_qk[:, g * QK:(g + 1) * QK],
+                        start=(g == 0), stop=(g == 1),
+                    )
+                    nc.tensor.matmul_mx(
+                        out=vb[:, tt * P:(tt + 1) * P],
+                        lhsT=xc[:, sl].bitcast(FP8X4), lhsT_scale=xs[:, sl],
+                        rhs=wc_v[:, g * P:(g + 1) * P].bitcast(FP8X4), rhs_scale=ws_v[:, g * P:(g + 1) * P],
+                        start=(g == 0), stop=(g == 1),
+                    )
+            qkbanks[r], vbanks[r] = qk, vb
+
+        def stored_with(r):
+            return (r, 1) if r >= ROUNDS - 2 else (r - r % 2, 2)
+
+        def stage_tile(kind, r):
+            first, count = stored_with(r)
+            if r == first:
+                st = stage.tile([P, H, 2 * RT, D], F32, name=kind, tag=kind)
+                stages[kind, first] = st
+            return stages[kind, first], (r - first) * RT
+
+        def store(dst, kind, r):
+            first, count = stored_with(r)
+            if r != first + count - 1:
+                return
+            b, j = divmod(first, RPB)
+            view = dst[b].rearrange("h (p t) d -> p h (t d)", t=TPB)
+            nt = count * RT
+            nc.sync.dma_start(
+                out=view[:, :, j * RT * D:(j * RT + nt) * D],
+                in_=stages[kind, first][:, :, 0:nt, :].rearrange("p h t d -> p h (t d)"),
+            )
+
+        def add_bias(r):
+            y = ypool.tile([P, RT, QK], F32, name="y", tag="y")
+            for half in range(2):
+                nc.vector.tensor_tensor(
+                    out=y[:, 2 * half:2 * half + 2, :],
+                    in0=qkbanks[r][half][:].rearrange("p (t c) -> p t c", t=2),
+                    in1=bias_qk[:].unsqueeze(1).to_broadcast([P, 2, QK]),
+                    op=ALU.add,
+                )
+            ys[r] = y
+            vst, tl = stage_tile("vst", r)
+            nc.vector.tensor_tensor(
+                out=vst[:, :, tl:tl + RT, :].rearrange("p h t d -> p t h d"),
+                in0=vbanks[r][:].rearrange("p (t h d) -> p t h d", t=RT, h=H),
+                in1=cv[:, 0:P].rearrange("p (h d) -> p h d", h=H).unsqueeze(1).to_broadcast([P, RT, H, D]),
+                op=ALU.add,
+            )
+            store(out_2, "vst", r)
+
+        def squares(r):
+            ss = small.tile([P, GROUPS], F32, name="ss", tag="ss")
+            sq = jpool.tile([P, GROUPS, D], F32, name="sq", tag="sq")
+            for n in range(GROUPS):
+                nc.scalar.activation(
+                    out=sq[:, n, :], in_=ys[r][:, n // 4, (n % 4) * D:(n % 4 + 1) * D],
+                    func=ACT.Square, accum_out=ss[:, n:n + 1],
+                )
+            rr = small.tile([P, GROUPS], F32, name="rr", tag="rr")
+            nc.scalar.activation(out=rr[:], in_=ss[:], func=ACT.Abs_reciprocal_sqrt, scale=1.0 / D, bias=eps[:])
+            rrs[r] = rr
+
+        def products(r):
+            t0 = (r % RPB) * RT
+            pr = ppool.tile([P, GROUPS, 2, D], F32, name="pr", tag="pr")
+            shape = [P, 2 * RT, H, 2, 2, PAIRS]
+            nc.vector.tensor_tensor(
+                out=pr[:].rearrange("p (m h) b (a i) -> p m h b a i", h=H, a=2),
+                in0=ys[r][:].rearrange("p t (s h b i) -> p (t s) h b i", s=2, h=H, b=2).unsqueeze(4).to_broadcast(shape),
+                in1=tab[:, t0:t0 + RT].rearrange("p t s b (a i) -> p (t s) b a i", a=2).unsqueeze(2).to_broadcast(shape),
+                op=ALU.mult,
+            )
+            prods[r] = pr
+
+        def pair_add(r):
+            sm = spool.tile([P, GROUPS, D], F32, name="sm", tag="sm")
+            pr = prods[r]
+            gn = GPSIMD_GROUPS_LAST if r == ROUNDS - 1 else GPSIMD_GROUPS
+            nc.gpsimd.tensor_tensor(out=sm[:, 0:gn, :], in0=pr[:, 0:gn, 0, :], in1=pr[:, 0:gn, 1, :], op=ALU.add)
+            nc.vector.tensor_tensor(out=sm[:, gn:, :], in0=pr[:, gn:, 0, :], in1=pr[:, gn:, 1, :], op=ALU.add)
+            sums[r] = sm
+
+        def scale_out(r):
+            qst, tl = stage_tile("qst", r)
+            kst, tl = stage_tile("kst", r)
+            sts = (qst, kst)
+            for n in range(GROUPS):
+                tt, s, h = n // 4, (n // 2) % 2, n % 2
+                dst = sts[s][:, h, tl + tt, :].rearrange("p (i a) -> p i a", a=2)
+                src = sums[r][:, n, :].rearrange("p (a i) -> p i a", a=2)
+                if r == ROUNDS - 1 and s == 1:
+                    nc.vector.tensor_scalar(out=dst, in0=src, scalar1=rrs[r][:, n:n + 1], scalar2=None, op0=ALU.mult)
+                else:
+                    nc.scalar.activation(out=dst, in_=src, func=ACT.Copy, scale=rrs[r][:, n:n + 1])
+            store(out_0, "qst", r)
+            store(out_1, "kst", r)
+
+        def live(r):
+            return 0 <= r < ROUNDS
+
+        transposes(0)
+        copy_out(0)
+        part = quantise(0, 2)
+        part(0)
+        table(0, 0)
+        part(1)
+        table(0, 1)
+        table(1, 0)
+        table(1, 1)
+        transposes(1)
+        project(0)
+        copy_out(1)
+        transposes(2)
+        copy_out(2)
+        transposes(3)
+        for i in range(0, ROUNDS + 1):
+            if live(i + 3):
+                copy_out(i + 3)
+            if i == 0:
+                add_bias(0)
+            if live(i + 1):
+                quantise(i + 1, 1)(0)
+            if live(i) and i > 0:
+                add_bias(i)
+            if live(i + 1):
+                project(i + 1)
+            if live(i + 4):
+                transposes(i + 4)
+            if live(i):
+                squares(i)
+            if live(i - 1):
+                pair_add(i - 1)
+                scale_out(i - 1)
+            if live(i):
+                products(i)

@@ -24,8 +24,8 @@ PAIRS = D // 2
 WORDS = DIM // 2
 BANK = 512
 NX = 6
-GPSIMD_GROUPS = 11
-GPSIMD_GROUPS_LAST = 5
+HALF = RT // 2
+TP_BANKS = 3
 FLOPS = 2 * B * L * DIM * 3 * H * D
 
 
@@ -38,17 +38,17 @@ def tile_selfattention_pa_t_kernel(tc, x, pe, qkv_w, qkv_b, q_scale, k_scale, ou
         cpool = ctx.enter_context(tc.tile_pool(name="cpool", bufs=2))
         ypool = ctx.enter_context(tc.tile_pool(name="ypool", bufs=2))
         ppool = ctx.enter_context(tc.tile_pool(name="ppool", bufs=2))
-        spool = ctx.enter_context(tc.tile_pool(name="spool", bufs=2))
         jpool = ctx.enter_context(tc.tile_pool(name="jpool", bufs=2))
         small = ctx.enter_context(tc.tile_pool(name="small", bufs=3))
         stage = ctx.enter_context(tc.tile_pool(name="stage", bufs=2))
-        psum_tp = ctx.enter_context(tc.psum_pool(name="psum_tp", bufs=4))
+        psum_tp = ctx.enter_context(tc.psum_pool(name="psum_tp", bufs=TP_BANKS))
         psum_qk = ctx.enter_context(tc.psum_pool(name="psum_qk", bufs=2))
-        psum_v = ctx.enter_context(tc.psum_pool(name="psum_v", bufs=2))
+        psum_v = ctx.enter_context(tc.psum_pool(name="psum_v", bufs=1))
+        psum_tab = ctx.enter_context(tc.psum_pool(name="psum_tab", bufs=2))
         ctx.enter_context(tc.manual_schedule())
 
-        xts, tps, groupeds, codes, planes = {}, {}, {}, {}, {}
-        qkbanks, vbanks, ys, prods, sums, rrs, stages = {}, {}, {}, {}, {}, {}, {}
+        xts, groupeds, codes, planes = {}, {}, {}, {}
+        qkbanks, vbanks, ys, tabs, prods, rrs, stages = {}, {}, {}, {}, {}, {}, {}
 
         def load(r):
             b, j = divmod(r, RPB)
@@ -115,38 +115,56 @@ def tile_selfattention_pa_t_kernel(tc, x, pe, qkv_w, qkv_b, q_scale, k_scale, ou
         cv = const.tile([P, QK], F32, name="cv", tag="cv")
         nc.vector.tensor_copy(out=cv[:], in_=cps[:, QK:BANK])
 
-        tab = const.tile([P, TPB, 2, 2, D], F32, name="tab", tag="tab")
-
-        def table(s, b):
-            gain = cv[:, P + s * D:P + (s + 1) * D].rearrange("p (i b) -> p b i", b=2)[:, b, :]
+        ident_bf = const.tile([P, P], BF16, name="ident_bf", tag="ident_bf")
+        nc.vector.tensor_copy(out=ident_bf[:], in_=ident[:])
+        diag = const.tile([P, 2 * P], BF16, name="diag", tag="diag")
+        for s in range(2):
             nc.vector.tensor_tensor(
-                out=tab[:, :, s, b, :].rearrange("p t (a i) -> p t a i", a=2),
-                in0=pe_sb[:].rearrange("p (t i a b) -> p t a i b", i=PAIRS, a=2, b=2)[:, :, :, :, b],
-                in1=gain.unsqueeze(1).unsqueeze(1).to_broadcast([P, TPB, 2, PAIRS]),
+                out=diag[:, s * P:(s + 1) * P].rearrange("p (b i a) -> p b i a", b=2, a=2),
+                in0=ident[:].rearrange("p (i a b) -> p b i a", a=2, b=2),
+                in1=cv[:, P + s * D:P + (s + 1) * D].rearrange("p (i b) -> p b i", b=2).unsqueeze(3).to_broadcast([P, 2, PAIRS, 2]),
                 op=ALU.mult,
             )
+        peT = const.tile([P, TPB, P], BF16, name="peT", tag="peT")
 
-        def transposes(r):
-            words = xts[r][:].bitcast(F32)
-            banks = []
+        def transpose_pe(j):
+            tp = psum_tp.tile([P, RT, P], BF16, name="tpe", tag="tp")
             for tt in range(RT):
+                t = j * RT + tt
+                nc.tensor.transpose(tp[:, tt, :], pe_sb[:, t * P:(t + 1) * P], ident_bf[:])
+            nc.scalar.copy(out=peT[:, j * RT:(j + 1) * RT, :], in_=tp[:])
+
+        def table(r, half):
+            tab = psum_tab.tile([P, HALF, 2 * P], F32, name="tab", tag="tab")
+            for k in range(HALF):
+                t = (r % RPB) * RT + half * HALF + k
+                nc.tensor.matmul(out=tab[:, k, :], lhsT=peT[:, t, :], rhs=diag[:], start=True, stop=True)
+            tabs[r, half] = tab
+
+        def transpose_x(r):
+            words = xts[r][:].bitcast(F32)
+            grouped = gpool.tile([P, RT * DIM], BF16, name="grouped", tag="grouped", align_bytes=64)
+            gw = grouped[:].bitcast(F32)
+            banks = {}
+
+            def copy_out(tt):
+                nc.scalar.copy(
+                    out=gw[:, tt * WORDS:(tt + 1) * WORDS].rearrange("p (g r u) -> p g r u", g=2, u=2),
+                    in_=banks[tt][:].rearrange("p (g u) r -> p g r u", u=2),
+                )
+
+            for tt in range(RT):
+                if tt >= TP_BANKS:
+                    copy_out(tt - TP_BANKS)
                 tp = psum_tp.tile([P, 4, P], F32, name="tp", tag="tp")
                 for c in range(4):
                     col = tt * WORDS + (c // 2) * 2 * P + c % 2
                     nc.tensor.transpose(tp[:, c, :], words[:, col:col + 2 * P - 1:2], ident[:])
-                banks.append(tp)
-            tps[r] = banks
+                banks[tt] = tp
+            for tt in range(RT - TP_BANKS, RT):
+                copy_out(tt)
             if r + NX < ROUNDS:
                 load(r + NX)
-
-        def copy_out(r):
-            grouped = gpool.tile([P, RT * DIM], BF16, name="grouped", tag="grouped", align_bytes=64)
-            gw = grouped[:].bitcast(F32)
-            for tt in range(RT):
-                nc.scalar.copy(
-                    out=gw[:, tt * WORDS:(tt + 1) * WORDS].rearrange("p (g r u) -> p g r u", g=2, u=2),
-                    in_=tps[r][tt][:].rearrange("p (g u) r -> p g r u", u=2),
-                )
             groupeds[r] = grouped
 
         def quantise(r, cuts):
@@ -191,14 +209,14 @@ def tile_selfattention_pa_t_kernel(tc, x, pe, qkv_w, qkv_b, q_scale, k_scale, ou
         def stored_with(r):
             return (r, 1) if r >= ROUNDS - 2 else (r - r % 2, 2)
 
-        def stage_tile(kind, r):
+        def stage_tile(kind, r, rows):
             first, count = stored_with(r)
-            if r == first:
-                st = stage.tile([P, H, 2 * RT, D], F32, name=kind, tag=kind)
+            if (kind, first) not in stages:
+                st = stage.tile([P, rows, 2 * RT, D], F32, name=kind, tag=kind)
                 stages[kind, first] = st
             return stages[kind, first], (r - first) * RT
 
-        def store(dst, kind, r):
+        def store(dst, kind, r, row):
             first, count = stored_with(r)
             if r != first + count - 1:
                 return
@@ -207,7 +225,7 @@ def tile_selfattention_pa_t_kernel(tc, x, pe, qkv_w, qkv_b, q_scale, k_scale, ou
             nt = count * RT
             nc.sync.dma_start(
                 out=view[:, :, j * RT * D:(j * RT + nt) * D],
-                in_=stages[kind, first][:, :, 0:nt, :].rearrange("p h t d -> p h (t d)"),
+                in_=stages[kind, first][:, row:row + H, 0:nt, :].rearrange("p h t d -> p h (t d)"),
             )
 
         def add_bias(r):
@@ -220,14 +238,14 @@ def tile_selfattention_pa_t_kernel(tc, x, pe, qkv_w, qkv_b, q_scale, k_scale, ou
                     op=ALU.add,
                 )
             ys[r] = y
-            vst, tl = stage_tile("vst", r)
+            vst, tl = stage_tile("vst", r, H)
             nc.vector.tensor_tensor(
                 out=vst[:, :, tl:tl + RT, :].rearrange("p h t d -> p t h d"),
                 in0=vbanks[r][:].rearrange("p (t h d) -> p t h d", t=RT, h=H),
                 in1=cv[:, 0:P].rearrange("p (h d) -> p h d", h=H).unsqueeze(1).to_broadcast([P, RT, H, D]),
                 op=ALU.add,
             )
-            store(out_2, "vst", r)
+            store(out_2, "vst", r, 0)
 
         def squares(r):
             ss = small.tile([P, GROUPS], F32, name="ss", tag="ss")
@@ -241,76 +259,62 @@ def tile_selfattention_pa_t_kernel(tc, x, pe, qkv_w, qkv_b, q_scale, k_scale, ou
             nc.scalar.activation(out=rr[:], in_=ss[:], func=ACT.Abs_reciprocal_sqrt, scale=1.0 / D, bias=eps[:])
             rrs[r] = rr
 
-        def products(r):
-            t0 = (r % RPB) * RT
-            pr = ppool.tile([P, GROUPS, 2, D], F32, name="pr", tag="pr")
-            shape = [P, 2 * RT, H, 2, 2, PAIRS]
-            nc.vector.tensor_tensor(
-                out=pr[:].rearrange("p (m h) b (a i) -> p m h b a i", h=H, a=2),
-                in0=ys[r][:].rearrange("p t (s h b i) -> p (t s) h b i", s=2, h=H, b=2).unsqueeze(4).to_broadcast(shape),
-                in1=tab[:, t0:t0 + RT].rearrange("p t s b (a i) -> p (t s) b a i", a=2).unsqueeze(2).to_broadcast(shape),
-                op=ALU.mult,
-            )
-            prods[r] = pr
+        def products(r, half):
+            if half == 0:
+                pr = ppool.tile([P, GROUPS, 2, D], F32, name="pr", tag="pr")
+                prods[r] = pr
+            for n in range(half * GROUPS // 2, (half + 1) * GROUPS // 2):
+                tt, s = n // 4, (n // 2) % 2
+                nc.vector.scalar_tensor_tensor(
+                    out=prods[r][:, n, :, :].rearrange("p b (i a) -> p (b i) a", a=2),
+                    in0=ys[r][:, tt, (n % 4) * D:(n % 4 + 1) * D].unsqueeze(2).to_broadcast([P, D, 2]),
+                    scalar=rrs[r][:, n:n + 1],
+                    in1=tabs[r, half][:, tt % HALF, s * P:(s + 1) * P].rearrange("p (c a) -> p c a", a=2),
+                    op0=ALU.mult, op1=ALU.mult,
+                )
 
-        def pair_add(r):
-            sm = spool.tile([P, GROUPS, D], F32, name="sm", tag="sm")
-            pr = prods[r]
-            gn = GPSIMD_GROUPS_LAST if r == ROUNDS - 1 else GPSIMD_GROUPS
-            nc.gpsimd.tensor_tensor(out=sm[:, 0:gn, :], in0=pr[:, 0:gn, 0, :], in1=pr[:, 0:gn, 1, :], op=ALU.add)
-            nc.vector.tensor_tensor(out=sm[:, gn:, :], in0=pr[:, gn:, 0, :], in1=pr[:, gn:, 1, :], op=ALU.add)
-            sums[r] = sm
-
-        def scale_out(r):
-            qst, tl = stage_tile("qst", r)
-            kst, tl = stage_tile("kst", r)
-            sts = (qst, kst)
-            for n in range(GROUPS):
-                tt, s, h = n // 4, (n // 2) % 2, n % 2
-                dst = sts[s][:, h, tl + tt, :].rearrange("p (i a) -> p i a", a=2)
-                src = sums[r][:, n, :].rearrange("p (a i) -> p i a", a=2)
-                if r == ROUNDS - 1 and s == 1:
-                    nc.vector.tensor_scalar(out=dst, in0=src, scalar1=rrs[r][:, n:n + 1], scalar2=None, op0=ALU.mult)
-                else:
-                    nc.scalar.activation(out=dst, in_=src, func=ACT.Copy, scale=rrs[r][:, n:n + 1])
-            store(out_0, "qst", r)
-            store(out_1, "kst", r)
+        def pair_add(r, half):
+            st, tl = stage_tile("qkst", r, 2 * H)
+            first = tl + half * HALF
+            pr = prods[r][:, half * GROUPS // 2:(half + 1) * GROUPS // 2].rearrange("p (t m) b d -> p t m b d", t=HALF)
+            out = st[:, :, first:first + HALF, :].rearrange("p m t d -> p t m d")
+            if r == ROUNDS - 1 and half == 1:
+                nc.gpsimd.tensor_tensor(out=out[:, 0], in0=pr[:, 0, :, 0, :], in1=pr[:, 0, :, 1, :], op=ALU.add)
+                nc.vector.tensor_tensor(out=out[:, 1], in0=pr[:, 1, :, 0, :], in1=pr[:, 1, :, 1, :], op=ALU.add)
+            else:
+                nc.gpsimd.tensor_tensor(out=out, in0=pr[:, :, :, 0, :], in1=pr[:, :, :, 1, :], op=ALU.add)
+            if half == 1:
+                store(out_0, "qkst", r, 0)
+                store(out_1, "qkst", r, H)
 
         def live(r):
             return 0 <= r < ROUNDS
 
-        transposes(0)
-        copy_out(0)
+        transpose_x(0)
         part = quantise(0, 2)
         part(0)
-        table(0, 0)
         part(1)
-        table(0, 1)
-        table(1, 0)
-        table(1, 1)
-        transposes(1)
+        transpose_x(1)
         project(0)
-        copy_out(1)
-        transposes(2)
-        copy_out(2)
-        transposes(3)
+        transpose_pe(0)
+        transpose_x(2)
         for i in range(0, ROUNDS + 1):
-            if live(i + 3):
-                copy_out(i + 3)
-            if i == 0:
-                add_bias(0)
-            if live(i + 1):
-                quantise(i + 1, 1)(0)
-            if live(i) and i > 0:
+            if live(i):
                 add_bias(i)
             if live(i + 1):
+                quantise(i + 1, 1)(0)
                 project(i + 1)
-            if live(i + 4):
-                transposes(i + 4)
             if live(i):
                 squares(i)
-            if live(i - 1):
-                pair_add(i - 1)
-                scale_out(i - 1)
+            for half in range(2):
+                if live(i - 1):
+                    products(i - 1, half)
+                    pair_add(i - 1, half)
             if live(i):
-                products(i)
+                table(i, 0)
+            if live(i + 3):
+                transpose_x(i + 3)
+            if live(i):
+                table(i, 1)
+            if 1 <= i + 1 < RPB:
+                transpose_pe(i + 1)

@@ -37,6 +37,7 @@ def tile_selfattention_pa_t_kernel(tc, x, pe, qkv_w, qkv_b, q_scale, k_scale, ou
         gpool = ctx.enter_context(tc.tile_pool(name="gpool", bufs=3))
         cpool = ctx.enter_context(tc.tile_pool(name="cpool", bufs=2))
         ypool = ctx.enter_context(tc.tile_pool(name="ypool", bufs=2))
+        spool = ctx.enter_context(tc.tile_pool(name="spool", bufs=2))
         ppool = ctx.enter_context(tc.tile_pool(name="ppool", bufs=2))
         jpool = ctx.enter_context(tc.tile_pool(name="jpool", bufs=2))
         small = ctx.enter_context(tc.tile_pool(name="small", bufs=3))
@@ -47,8 +48,8 @@ def tile_selfattention_pa_t_kernel(tc, x, pe, qkv_w, qkv_b, q_scale, k_scale, ou
         psum_tab = ctx.enter_context(tc.psum_pool(name="psum_tab", bufs=2))
         ctx.enter_context(tc.manual_schedule())
 
-        xts, groupeds, codes, planes = {}, {}, {}, {}
-        qkbanks, vbanks, ys, tabs, prods, rrs, stages = {}, {}, {}, {}, {}, {}, {}
+        xts, tps, groupeds, codes, planes = {}, {}, {}, {}, {}
+        qkbanks, vbanks, ys, tabs, prods, sums, rrs, stages = {}, {}, {}, {}, {}, {}, {}, {}
 
         def load(r):
             b, j = divmod(r, RPB)
@@ -141,31 +142,24 @@ def tile_selfattention_pa_t_kernel(tc, x, pe, qkv_w, qkv_b, q_scale, k_scale, ou
                 nc.tensor.matmul(out=tab[:, k, :], lhsT=peT[:, t, :], rhs=diag[:], start=True, stop=True)
             tabs[r, half] = tab
 
-        def transpose_x(r):
+        def transposes(r, tt):
             words = xts[r][:].bitcast(F32)
-            grouped = gpool.tile([P, RT * DIM], BF16, name="grouped", tag="grouped", align_bytes=64)
-            gw = grouped[:].bitcast(F32)
-            banks = {}
-
-            def copy_out(tt):
-                nc.scalar.copy(
-                    out=gw[:, tt * WORDS:(tt + 1) * WORDS].rearrange("p (g r u) -> p g r u", g=2, u=2),
-                    in_=banks[tt][:].rearrange("p (g u) r -> p g r u", u=2),
-                )
-
-            for tt in range(RT):
-                if tt >= TP_BANKS:
-                    copy_out(tt - TP_BANKS)
-                tp = psum_tp.tile([P, 4, P], F32, name="tp", tag="tp")
-                for c in range(4):
-                    col = tt * WORDS + (c // 2) * 2 * P + c % 2
-                    nc.tensor.transpose(tp[:, c, :], words[:, col:col + 2 * P - 1:2], ident[:])
-                banks[tt] = tp
-            for tt in range(RT - TP_BANKS, RT):
-                copy_out(tt)
-            if r + NX < ROUNDS:
+            tp = psum_tp.tile([P, 4, P], F32, name="tp", tag="tp")
+            for c in range(4):
+                col = tt * WORDS + (c // 2) * 2 * P + c % 2
+                nc.tensor.transpose(tp[:, c, :], words[:, col:col + 2 * P - 1:2], ident[:])
+            tps[r, tt] = tp
+            if tt == RT - 1 and r + NX < ROUNDS:
                 load(r + NX)
-            groupeds[r] = grouped
+
+        def copy_out(r, tt):
+            if tt == 0:
+                grouped = gpool.tile([P, RT * DIM], BF16, name="grouped", tag="grouped", align_bytes=64)
+                groupeds[r] = grouped
+            nc.scalar.copy(
+                out=groupeds[r][:].bitcast(F32)[:, tt * WORDS:(tt + 1) * WORDS].rearrange("p (g r u) -> p g r u", g=2, u=2),
+                in_=tps[r, tt][:].rearrange("p (g u) r -> p g r u", u=2),
+            )
 
         def quantise(r, cuts):
             xc = cpool.tile([P, RT * 2 * P], U32, name="xc", tag="xc", align_bytes=64)
@@ -263,26 +257,39 @@ def tile_selfattention_pa_t_kernel(tc, x, pe, qkv_w, qkv_b, q_scale, k_scale, ou
             if half == 0:
                 pr = ppool.tile([P, GROUPS, 2, D], F32, name="pr", tag="pr")
                 prods[r] = pr
-            for n in range(half * GROUPS // 2, (half + 1) * GROUPS // 2):
-                tt, s = n // 4, (n // 2) % 2
-                nc.vector.scalar_tensor_tensor(
-                    out=prods[r][:, n, :, :].rearrange("p b (i a) -> p (b i) a", a=2),
-                    in0=ys[r][:, tt, (n % 4) * D:(n % 4 + 1) * D].unsqueeze(2).to_broadcast([P, D, 2]),
-                    scalar=rrs[r][:, n:n + 1],
-                    in1=tabs[r, half][:, tt % HALF, s * P:(s + 1) * P].rearrange("p (c a) -> p c a", a=2),
-                    op0=ALU.mult, op1=ALU.mult,
-                )
+            shape = [P, 2 * HALF, H, D, 2]
+            nc.vector.tensor_tensor(
+                out=prods[r][:, half * GROUPS // 2:(half + 1) * GROUPS // 2].rearrange("p (m h) b (i a) -> p m h (b i) a", h=H, a=2),
+                in0=ys[r][:, half * HALF:(half + 1) * HALF, :].rearrange("p t (s h c) -> p (t s) h c", s=2, h=H).unsqueeze(4).to_broadcast(shape),
+                in1=tabs[r, half][:].rearrange("p t (s c a) -> p (t s) c a", s=2, a=2).unsqueeze(2).to_broadcast(shape),
+                op=ALU.mult,
+            )
 
         def pair_add(r, half):
-            st, tl = stage_tile("qkst", r, 2 * H)
-            first = tl + half * HALF
-            pr = prods[r][:, half * GROUPS // 2:(half + 1) * GROUPS // 2].rearrange("p (t m) b d -> p t m b d", t=HALF)
-            out = st[:, :, first:first + HALF, :].rearrange("p m t d -> p t m d")
+            if half == 0:
+                sm = spool.tile([P, GROUPS, D], F32, name="sm", tag="sm")
+                sums[r] = sm
+            first, last = half * GROUPS // 2, (half + 1) * GROUPS // 2
             if r == ROUNDS - 1 and half == 1:
-                nc.gpsimd.tensor_tensor(out=out[:, 0], in0=pr[:, 0, :, 0, :], in1=pr[:, 0, :, 1, :], op=ALU.add)
-                nc.vector.tensor_tensor(out=out[:, 1], in0=pr[:, 1, :, 0, :], in1=pr[:, 1, :, 1, :], op=ALU.add)
-            else:
-                nc.gpsimd.tensor_tensor(out=out, in0=pr[:, :, :, 0, :], in1=pr[:, :, :, 1, :], op=ALU.add)
+                mid = (first + last) // 2
+                nc.vector.tensor_tensor(
+                    out=sums[r][:, mid:last, :], in0=prods[r][:, mid:last, 0, :], in1=prods[r][:, mid:last, 1, :], op=ALU.add,
+                )
+                last = mid
+            nc.gpsimd.tensor_tensor(
+                out=sums[r][:, first:last, :], in0=prods[r][:, first:last, 0, :], in1=prods[r][:, first:last, 1, :], op=ALU.add,
+            )
+
+        def scale_out(r, half):
+            st, tl = stage_tile("qkst", r, 2 * H)
+            for n in range(half * GROUPS // 2, (half + 1) * GROUPS // 2):
+                tt, m = divmod(n, 2 * H)
+                if r == ROUNDS - 1 and n % 2 == 1:
+                    nc.vector.tensor_scalar(
+                        out=st[:, m, tl + tt, :], in0=sums[r][:, n, :], scalar1=rrs[r][:, n:n + 1], scalar2=None, op0=ALU.mult,
+                    )
+                else:
+                    nc.scalar.activation(out=st[:, m, tl + tt, :], in_=sums[r][:, n, :], func=ACT.Copy, scale=rrs[r][:, n:n + 1])
             if half == 1:
                 store(out_0, "qkst", r, 0)
                 store(out_1, "qkst", r, H)
@@ -290,31 +297,51 @@ def tile_selfattention_pa_t_kernel(tc, x, pe, qkv_w, qkv_b, q_scale, k_scale, ou
         def live(r):
             return 0 <= r < ROUNDS
 
-        transpose_x(0)
+        def transpose_round(r):
+            for tt in range(RT):
+                if tt >= TP_BANKS:
+                    copy_out(r, tt - TP_BANKS)
+                transposes(r, tt)
+            for tt in range(RT - TP_BANKS, RT):
+                copy_out(r, tt)
+
+        transpose_round(0)
         part = quantise(0, 2)
         part(0)
         part(1)
-        transpose_x(1)
+        transpose_round(1)
         project(0)
         transpose_pe(0)
-        transpose_x(2)
-        for i in range(0, ROUNDS + 1):
+        for tt in range(TP_BANKS):
+            transposes(2, tt)
+        for i in range(0, ROUNDS + 2):
+            if live(i - 2):
+                scale_out(i - 2, 0)
+            if live(i + 2):
+                copy_out(i + 2, 0)
+                transposes(i + 2, RT - 1)
             if live(i):
                 add_bias(i)
+            if live(i - 2):
+                scale_out(i - 2, 1)
             if live(i + 1):
                 quantise(i + 1, 1)(0)
                 project(i + 1)
             if live(i):
                 squares(i)
+            if live(i + 2):
+                for tt in range(1, RT):
+                    copy_out(i + 2, tt)
             for half in range(2):
                 if live(i - 1):
                     products(i - 1, half)
                     pair_add(i - 1, half)
             if live(i):
                 table(i, 0)
-            if live(i + 3):
-                transpose_x(i + 3)
-            if live(i):
-                table(i, 1)
             if 1 <= i + 1 < RPB:
                 transpose_pe(i + 1)
+            if live(i + 3):
+                for tt in range(TP_BANKS):
+                    transposes(i + 3, tt)
+            if live(i):
+                table(i, 1)

@@ -282,14 +282,22 @@ def tile_selfattention_pa_t_kernel(tc, x, pe, qkv_w, qkv_b, q_scale, k_scale, ou
 
         def scale_out(r, half):
             st, tl = stage_tile("qkst", r, 2 * H)
-            for n in range(half * GROUPS // 2, (half + 1) * GROUPS // 2):
-                tt, m = divmod(n, 2 * H)
-                if r == ROUNDS - 1 and n % 2 == 1:
-                    nc.vector.tensor_scalar(
-                        out=st[:, m, tl + tt, :], in0=sums[r][:, n, :], scalar1=rrs[r][:, n:n + 1], scalar2=None, op0=ALU.mult,
-                    )
-                else:
-                    nc.scalar.activation(out=st[:, m, tl + tt, :], in_=sums[r][:, n, :], func=ACT.Copy, scale=rrs[r][:, n:n + 1])
+            if half == 1 and r < ROUNDS - 1:
+                nc.gpsimd.tensor_tensor(
+                    out=st[:, :, tl + HALF:tl + RT, :].rearrange("p m t d -> p t m d"),
+                    in0=sums[r][:, GROUPS // 2:, :].rearrange("p (t m) d -> p t m d", t=HALF),
+                    in1=rrs[r][:, GROUPS // 2:].rearrange("p (t m) -> p t m", t=HALF).unsqueeze(3).to_broadcast([P, HALF, 2 * H, D]),
+                    op=ALU.mult,
+                )
+            else:
+                for n in range(half * GROUPS // 2, (half + 1) * GROUPS // 2):
+                    tt, m = divmod(n, 2 * H)
+                    if r == ROUNDS - 1 and n % 2 == 1:
+                        nc.vector.tensor_scalar(
+                            out=st[:, m, tl + tt, :], in0=sums[r][:, n, :], scalar1=rrs[r][:, n:n + 1], scalar2=None, op0=ALU.mult,
+                        )
+                    else:
+                        nc.scalar.activation(out=st[:, m, tl + tt, :], in_=sums[r][:, n, :], func=ACT.Copy, scale=rrs[r][:, n:n + 1])
             if half == 1:
                 store(out_0, "qkst", r, 0)
                 store(out_1, "qkst", r, H)
@@ -315,33 +323,35 @@ def tile_selfattention_pa_t_kernel(tc, x, pe, qkv_w, qkv_b, q_scale, k_scale, ou
         for tt in range(TP_BANKS):
             transposes(2, tt)
         for i in range(0, ROUNDS + 2):
-            if live(i - 2):
-                scale_out(i - 2, 0)
             if live(i + 2):
                 copy_out(i + 2, 0)
                 transposes(i + 2, RT - 1)
-            if live(i):
-                add_bias(i)
-            if live(i - 2):
-                scale_out(i - 2, 1)
+                for tt in range(1, RT - 1):
+                    copy_out(i + 2, tt)
+            if i == 0:
+                add_bias(0)
             if live(i + 1):
                 quantise(i + 1, 1)(0)
                 project(i + 1)
+            if live(i) and i > 0:
+                add_bias(i)
+            if live(i - 2):
+                pair_add(i - 2, 0)
+                pair_add(i - 2, 1)
             if live(i):
                 squares(i)
+            if live(i - 2):
+                scale_out(i - 2, 0)
+                scale_out(i - 2, 1)
             if live(i + 2):
-                for tt in range(1, RT):
-                    copy_out(i + 2, tt)
-            for half in range(2):
-                if live(i - 1):
-                    products(i - 1, half)
-                    pair_add(i - 1, half)
-            if live(i):
-                table(i, 0)
+                copy_out(i + 2, RT - 1)
             if 1 <= i + 1 < RPB:
                 transpose_pe(i + 1)
             if live(i + 3):
                 for tt in range(TP_BANKS):
                     transposes(i + 3, tt)
-            if live(i):
-                table(i, 1)
+            for half in range(2):
+                if live(i - 1):
+                    products(i - 1, half)
+                if live(i):
+                    table(i, half)

@@ -15,17 +15,18 @@ B, L, DIM, H, D = 4, 2048, 1024, 2, 64
 EPS = 1e-6
 P = 128
 TPB = L // P
-RT = 4
-RPB = TPB // RT
-ROUNDS = B * RPB
-GROUPS = RT * 2 * H
-QK = 2 * H * D
+CT = 2
+CPB = TPB // CT
+CHUNKS = B * CPB
+ROWS = 2 * H
+GROUPS = CT * ROWS
+QK = ROWS * D
 PAIRS = D // 2
 WORDS = DIM // 2
 BANK = 512
+LC = 2
 NX = 6
-HALF = RT // 2
-TP_BANKS = 3
+SCALAR_GROUPS = 6
 FLOPS = 2 * B * L * DIM * 3 * H * D
 
 
@@ -35,61 +36,211 @@ def tile_selfattention_pa_t_kernel(tc, x, pe, qkv_w, qkv_b, q_scale, k_scale, ou
         const = ctx.enter_context(tc.tile_pool(name="const", bufs=1))
         xpool = ctx.enter_context(tc.tile_pool(name="xpool", bufs=NX))
         gpool = ctx.enter_context(tc.tile_pool(name="gpool", bufs=3))
-        cpool = ctx.enter_context(tc.tile_pool(name="cpool", bufs=2))
-        ypool = ctx.enter_context(tc.tile_pool(name="ypool", bufs=2))
-        spool = ctx.enter_context(tc.tile_pool(name="spool", bufs=2))
-        ppool = ctx.enter_context(tc.tile_pool(name="ppool", bufs=2))
+        cpool = ctx.enter_context(tc.tile_pool(name="cpool", bufs=3))
+        ypool = ctx.enter_context(tc.tile_pool(name="ypool", bufs=3))
+        ppool = ctx.enter_context(tc.tile_pool(name="ppool", bufs=3))
+        spool = ctx.enter_context(tc.tile_pool(name="spool", bufs=3))
         jpool = ctx.enter_context(tc.tile_pool(name="jpool", bufs=2))
-        small = ctx.enter_context(tc.tile_pool(name="small", bufs=3))
-        stage = ctx.enter_context(tc.tile_pool(name="stage", bufs=2))
-        psum_tp = ctx.enter_context(tc.psum_pool(name="psum_tp", bufs=TP_BANKS))
+        small = ctx.enter_context(tc.tile_pool(name="small", bufs=4))
+        stage = ctx.enter_context(tc.tile_pool(name="stage", bufs=3))
+        psum_tp = ctx.enter_context(tc.psum_pool(name="psum_tp", bufs=2))
         psum_qk = ctx.enter_context(tc.psum_pool(name="psum_qk", bufs=2))
-        psum_v = ctx.enter_context(tc.psum_pool(name="psum_v", bufs=1))
+        psum_v = ctx.enter_context(tc.psum_pool(name="psum_v", bufs=2))
         psum_tab = ctx.enter_context(tc.psum_pool(name="psum_tab", bufs=2))
         ctx.enter_context(tc.manual_schedule())
 
-        xts, tps, groupeds, codes, planes = {}, {}, {}, {}, {}
+        xts, tps, groupeds, codes = {}, {}, {}, {}
         qkbanks, vbanks, ys, tabs, prods, sums, rrs, stages = {}, {}, {}, {}, {}, {}, {}, {}
 
-        def load(r):
-            b, j = divmod(r, RPB)
-            xt = xpool.tile([P, RT * DIM], BF16, name="xt", tag="xt")
+        def load(m, cuts=1, part=0):
+            b, j = divmod(m, CPB // LC)
+            if part == 0:
+                xt = xpool.tile([P, LC * CT * DIM], BF16, name="xt", tag="xt")
+                xts[m] = xt
             src = x[b].rearrange("(p t) k -> p (t k)", t=TPB)
-            first = j * RT * DIM
-            cuts = 2 if r == 0 else 1
-            width = RT * DIM // cuts
-            for c in range(cuts):
-                nc.sync.dma_start(
-                    out=xt[:, c * width:(c + 1) * width],
-                    in_=src[:, first + c * width:first + (c + 1) * width],
-                )
-            xts[r] = xt
+            width = LC * CT * DIM // cuts
+            first = j * LC * CT * DIM + part * width
+            nc.sync.dma_start(out=xts[m][:, part * width:(part + 1) * width], in_=src[:, first:first + width])
 
-        ident = const.tile([P, P], F32, name="ident", tag="ident")
-        make_identity(nc, ident[:])
-        ones = const.tile([P, P], BF16, name="ones", tag="ones")
-        nc.vector.memset(ones[:], 1.0)
-        row = const.tile([P, BANK], BF16, name="row", tag="row")
-        nc.vector.memset(row[:], 0.0)
-        eps = const.tile([P, 1], F32, name="eps", tag="eps")
-        nc.vector.memset(eps[:], EPS)
-        junk = const.tile([P, D], F32, name="junk", tag="junk")
-
+        load(0, 4, 0)
+        load(0, 4, 1)
         w_raw = const.tile([P, 8, 3 * P], BF16, name="w_raw", tag="w_raw")
         nc.sync.dma_start(
             out=w_raw[:].rearrange("p (g t) n -> p g (t n)", t=4),
             in_=qkv_w.rearrange("(g q t) n -> q g (t n)", g=2, t=4),
         )
+        row = const.tile([P, BANK], BF16, name="row", tag="row")
+        nc.vector.memset(row[:], 0.0)
         nc.sync.dma_start(out=row[0:1, 0:3 * P], in_=qkv_b.unsqueeze(0))
         nc.sync.dma_start(out=row[0:1, 3 * P:3 * P + D], in_=q_scale.unsqueeze(0))
         nc.sync.dma_start(out=row[0:1, 3 * P + D:BANK], in_=k_scale.unsqueeze(0))
-        load(0)
-        pe_sb = const.tile([P, TPB * 4 * PAIRS], BF16, name="pe_sb", tag="pe_sb")
-        nc.sync.dma_start(out=pe_sb[:], in_=pe[0, 0].rearrange("(p t) i a b -> p (t i a b)", t=TPB))
-        for r in range(1, NX):
-            load(r)
-        nc.scalar.activation(out=junk[:, 0:1], in_=eps[:], func=ACT.Abs_reciprocal_sqrt)
+        load(0, 2, 1)
+        pe_sb = const.tile([P, TPB * P], BF16, name="pe_sb", tag="pe_sb")
+        pe_src = pe[0, 0].rearrange("(p t) i a b -> p (t i a b)", t=TPB)
+        nc.sync.dma_start(out=pe_sb[:, 0:4 * P], in_=pe_src[:, 0:4 * P])
+        load(1)
+        nc.sync.dma_start(out=pe_sb[:, 4 * P:], in_=pe_src[:, 4 * P:])
+        for m in range(2, NX):
+            load(m)
 
+        ident = const.tile([P, P], F32, name="ident", tag="ident")
+        make_identity(nc, ident[:])
+        ones = const.tile([P, P], BF16, name="ones", tag="ones")
+        nc.vector.memset(ones[:], 1.0)
+        eps = const.tile([P, 1], F32, name="eps", tag="eps")
+        nc.vector.memset(eps[:], EPS)
+        ident_bf = const.tile([P, P], BF16, name="ident_bf", tag="ident_bf")
+        nc.vector.tensor_copy(out=ident_bf[:], in_=ident[:])
+        junk = const.tile([P, 1], F32, name="junk", tag="junk")
+        nc.scalar.activation(out=junk[:], in_=eps[:], func=ACT.Abs_reciprocal_sqrt)
+
+        def transposes(h):
+            words = xts[h // LC][:].bitcast(F32)
+            for tt in range(CT):
+                tp = psum_tp.tile([P, 4, P], F32, name="tp", tag="tp")
+                for c in range(4):
+                    col = (h % LC * CT + tt) * WORDS + (c // 2) * 2 * P + c % 2
+                    nc.tensor.transpose(tp[:, c, :], words[:, col:col + 2 * P - 1:2], ident[:])
+                tps[h, tt] = tp
+            if h % LC == LC - 1 and h // LC + NX < CHUNKS // LC:
+                load(h // LC + NX)
+
+        def copy_out(h):
+            grouped = gpool.tile([P, CT * DIM], BF16, name="grouped", tag="grouped", align_bytes=64)
+            groupeds[h] = grouped
+            for tt in range(CT):
+                nc.scalar.copy(
+                    out=grouped[:].bitcast(F32)[:, tt * WORDS:(tt + 1) * WORDS].rearrange("p (g r u) -> p g r u", g=2, u=2),
+                    in_=tps[h, tt][:].rearrange("p (g u) r -> p g r u", u=2),
+                )
+
+        def quantise(h):
+            xc = cpool.tile([P, CT * 2 * P], U32, name="xc", tag="xc", align_bytes=64)
+            xs = cpool.tile([P, CT * 2 * P], U8, name="xs", tag="xs", align_bytes=64)
+            nc.vector.quantize_mx(out=xc[:].bitcast(FP8X4), scales=xs[:], in_=groupeds[h][:])
+            codes[h] = xc, xs
+
+        def project(h):
+            xc, xs = codes[h]
+            qkb = psum_qk.tile([P, CT * QK], F32, name="qkb", tag="qkb")
+            vb = psum_v.tile([P, CT * P], F32, name="vb", tag="vb")
+            for bank, width, wc, ws in ((qkb, QK, wc_qk, ws_qk), (vb, P, wc_v, ws_v)):
+                for tt in range(CT):
+                    for g in range(2):
+                        sl = slice((tt * 2 + g) * P, (tt * 2 + g + 1) * P)
+                        nc.tensor.matmul_mx(
+                            out=bank[:, tt * width:(tt + 1) * width],
+                            lhsT=xc[:, sl].bitcast(FP8X4), lhsT_scale=xs[:, sl],
+                            rhs=wc[:, g * width:(g + 1) * width].bitcast(FP8X4), rhs_scale=ws[:, g * width:(g + 1) * width],
+                            start=(g == 0), stop=(g == 1),
+                        )
+            qkbanks[h], vbanks[h] = qkb, vb
+
+        def stored_with(h):
+            if h >= CHUNKS - 2:
+                return h, 1
+            if h >= CHUNKS - 4:
+                return CHUNKS - 4, 2
+            return h - h % 4, 4
+
+        def stage_tile(kind, h, rows):
+            first, count = stored_with(h)
+            if (kind, first) not in stages:
+                st = stage.tile([P, rows, 4 * CT, D], F32, name=kind, tag=kind)
+                stages[kind, first] = st
+            return stages[kind, first], (h - first) * CT
+
+        def store(dst, kind, h, row):
+            first, count = stored_with(h)
+            if h != first + count - 1:
+                return
+            b, j = divmod(first, CPB)
+            view = dst[b].rearrange("h (p t) d -> p h (t d)", t=TPB)
+            nt = count * CT
+            nc.sync.dma_start(
+                out=view[:, :, j * CT * D:(j * CT + nt) * D],
+                in_=stages[kind, first][:, row:row + H, 0:nt, :].rearrange("p h t d -> p h (t d)"),
+            )
+
+        def add_bias(h):
+            y = ypool.tile([P, CT, QK], F32, name="y", tag="y")
+            nc.vector.tensor_tensor(
+                out=y[:],
+                in0=qkbanks[h][:].rearrange("p (t c) -> p t c", t=CT),
+                in1=bias_qk[:].unsqueeze(1).to_broadcast([P, CT, QK]),
+                op=ALU.add,
+            )
+            ys[h] = y
+            vst, tl = stage_tile("vst", h, H)
+            nc.vector.tensor_tensor(
+                out=vst[:, :, tl:tl + CT, :].rearrange("p h t d -> p t h d"),
+                in0=vbanks[h][:].rearrange("p (t h d) -> p t h d", t=CT, h=H),
+                in1=cv[:, 0:P].rearrange("p (h d) -> p h d", h=H).unsqueeze(1).to_broadcast([P, CT, H, D]),
+                op=ALU.add,
+            )
+            store(out_2, "vst", h, 0)
+
+        def squares(h):
+            ss = small.tile([P, GROUPS], F32, name="ss", tag="ss")
+            sq = jpool.tile([P, GROUPS, D], F32, name="sq", tag="sq")
+            for n in range(GROUPS):
+                tt, m = divmod(n, ROWS)
+                nc.scalar.activation(
+                    out=sq[:, n, :], in_=ys[h][:, tt, m * D:(m + 1) * D], func=ACT.Square, accum_out=ss[:, n:n + 1],
+                )
+            rr = small.tile([P, GROUPS], F32, name="rr", tag="rr")
+            nc.scalar.activation(out=rr[:], in_=ss[:], func=ACT.Abs_reciprocal_sqrt, scale=1.0 / D, bias=eps[:])
+            rrs[h] = rr
+
+        def table(h):
+            tab = psum_tab.tile([P, CT, 2 * P], F32, name="tab", tag="tab")
+            for tt in range(CT):
+                t = h % CPB * CT + tt
+                nc.tensor.matmul(out=tab[:, tt, :], lhsT=pe_t[:, t, :], rhs=diag[:], start=True, stop=True)
+            tabs[h] = tab
+
+        def products(h):
+            pr = ppool.tile([P, GROUPS, 2, D], F32, name="pr", tag="pr")
+            shape = [P, CT * 2, H, D, 2]
+            nc.vector.tensor_tensor(
+                out=pr[:].rearrange("p (m h) b (i a) -> p m h (b i) a", h=H, a=2),
+                in0=ys[h][:].rearrange("p t (s h c) -> p (t s) h c", s=2, h=H).unsqueeze(4).to_broadcast(shape),
+                in1=tabs[h][:].rearrange("p t (s c a) -> p (t s) c a", s=2, a=2).unsqueeze(2).to_broadcast(shape),
+                op=ALU.mult,
+            )
+            prods[h] = pr
+
+        def pair_add(h):
+            sm = spool.tile([P, GROUPS, D], F32, name="sm", tag="sm")
+            sums[h] = sm
+            gn = GROUPS // 2 if h == CHUNKS - 1 else GROUPS
+            pr = prods[h]
+            if gn < GROUPS:
+                nc.vector.tensor_tensor(out=sm[:, gn:, :], in0=pr[:, gn:, 0, :], in1=pr[:, gn:, 1, :], op=ALU.add)
+            nc.gpsimd.tensor_tensor(out=sm[:, 0:gn, :], in0=pr[:, 0:gn, 0, :], in1=pr[:, 0:gn, 1, :], op=ALU.add)
+
+        def scale_out(h):
+            st, tl = stage_tile("qkst", h, ROWS)
+            sm, rr = sums[h], rrs[h]
+            last = h == CHUNKS - 1
+            if not last:
+                nc.gpsimd.tensor_tensor(
+                    out=st[:, SCALAR_GROUPS - ROWS:, tl + 1, :],
+                    in0=sm[:, SCALAR_GROUPS:, :],
+                    in1=rr[:, SCALAR_GROUPS:].unsqueeze(2).to_broadcast([P, GROUPS - SCALAR_GROUPS, D]),
+                    op=ALU.mult,
+                )
+            for n in range(GROUPS if last else SCALAR_GROUPS):
+                tt, m = divmod(n, ROWS)
+                if last and tt == 1:
+                    nc.vector.tensor_scalar(out=st[:, m, tl + tt, :], in0=sm[:, n, :], scalar1=rr[:, n:n + 1], scalar2=None, op0=ALU.mult)
+                else:
+                    nc.scalar.activation(out=st[:, m, tl + tt, :], in_=sm[:, n, :], func=ACT.Copy, scale=rr[:, n:n + 1])
+            store(out_0, "qkst", h, 0)
+            store(out_1, "qkst", h, H)
+
+        transposes(0)
+        copy_out(0)
         wg_qk = const.tile([P, 2, QK, 4], BF16, name="wg_qk", tag="wg_qk", align_bytes=64)
         wg_v = const.tile([P, 2, P, 4], BF16, name="wg_v", tag="wg_v", align_bytes=64)
         for g in range(2):
@@ -98,260 +249,66 @@ def tile_selfattention_pa_t_kernel(tc, x, pe, qkv_w, qkv_b, q_scale, k_scale, ou
                     out=wg_qk[:, g].rearrange("p (n b i) t -> p n b i t", n=4, b=2)[:, :, b],
                     in_=w_raw[:, 4 * g:4 * g + 4, 0:QK].rearrange("p t (n i b) -> p n i t b", i=PAIRS, b=2)[:, :, :, :, b],
                 )
-            nc.scalar.copy(out=wg_v[:, g], in_=w_raw[:, 4 * g:4 * g + 4, QK:3 * P].rearrange("p t n -> p n t"))
+        for g in range(2):
+            nc.vector.tensor_copy(out=wg_v[:, g], in_=w_raw[:, 4 * g:4 * g + 4, QK:3 * P].rearrange("p t n -> p n t"))
         wc_qk = const.tile([P, 2 * QK], U32, name="wc_qk", tag="wc_qk", align_bytes=64)
         ws_qk = const.tile([P, 2 * QK], U8, name="ws_qk", tag="ws_qk", align_bytes=64)
         wc_v = const.tile([P, 2 * P], U32, name="wc_v", tag="wc_v", align_bytes=64)
         ws_v = const.tile([P, 2 * P], U8, name="ws_v", tag="ws_v", align_bytes=64)
         nc.vector.quantize_mx(out=wc_qk[:].bitcast(FP8X4), scales=ws_qk[:], in_=wg_qk[:].rearrange("p g n t -> p (g n t)"))
+        quantise(0)
         nc.vector.quantize_mx(out=wc_v[:].bitcast(FP8X4), scales=ws_v[:], in_=wg_v[:].rearrange("p g n t -> p (g n t)"))
 
-        cps = psum_v.tile([P, BANK], F32, name="cps", tag="vb")
+        cps = psum_tab.tile([P, BANK], F32, name="cps", tag="tab")
         nc.tensor.matmul(out=cps[:], lhsT=ones[:], rhs=row[:], start=True, stop=True)
         bias_qk = const.tile([P, QK], F32, name="bias_qk", tag="bias_qk")
-        nc.vector.tensor_copy(
+        nc.scalar.copy(
             out=bias_qk[:].rearrange("p (n b i) -> p n b i", b=2, i=PAIRS),
             in_=cps[:, 0:QK].rearrange("p (n i b) -> p n b i", i=PAIRS, b=2),
         )
         cv = const.tile([P, QK], F32, name="cv", tag="cv")
-        nc.vector.tensor_copy(out=cv[:], in_=cps[:, QK:BANK])
+        nc.scalar.copy(out=cv[:], in_=cps[:, QK:BANK])
 
-        ident_bf = const.tile([P, P], BF16, name="ident_bf", tag="ident_bf")
-        nc.vector.tensor_copy(out=ident_bf[:], in_=ident[:])
         diag = const.tile([P, 2 * P], BF16, name="diag", tag="diag")
         for s in range(2):
-            nc.vector.tensor_tensor(
+            nc.gpsimd.tensor_tensor(
                 out=diag[:, s * P:(s + 1) * P].rearrange("p (b i a) -> p b i a", b=2, a=2),
                 in0=ident[:].rearrange("p (i a b) -> p b i a", a=2, b=2),
                 in1=cv[:, P + s * D:P + (s + 1) * D].rearrange("p (i b) -> p b i", b=2).unsqueeze(3).to_broadcast([P, 2, PAIRS, 2]),
                 op=ALU.mult,
             )
-        peT = const.tile([P, TPB, P], BF16, name="peT", tag="peT")
+        pe_t = const.tile([P, TPB, P], BF16, name="pe_t", tag="pe_t")
 
         def transpose_pe(j):
-            tp = psum_tp.tile([P, RT, P], BF16, name="tpe", tag="tp")
-            for tt in range(RT):
-                t = j * RT + tt
-                nc.tensor.transpose(tp[:, tt, :], pe_sb[:, t * P:(t + 1) * P], ident_bf[:])
-            nc.scalar.copy(out=peT[:, j * RT:(j + 1) * RT, :], in_=tp[:])
+            tp = psum_tp.tile([P, 4, P], BF16, name="tpe", tag="tp")
+            for t in range(4):
+                nc.tensor.transpose(tp[:, t, :], pe_sb[:, (4 * j + t) * P:(4 * j + t + 1) * P], ident_bf[:])
+            nc.scalar.copy(out=pe_t[:, 4 * j:4 * j + 4, :], in_=tp[:])
 
-        def table(r, half):
-            tab = psum_tab.tile([P, HALF, 2 * P], F32, name="tab", tag="tab")
-            for k in range(HALF):
-                t = (r % RPB) * RT + half * HALF + k
-                nc.tensor.matmul(out=tab[:, k, :], lhsT=peT[:, t, :], rhs=diag[:], start=True, stop=True)
-            tabs[r, half] = tab
+        def live(h):
+            return 0 <= h < CHUNKS
 
-        def transposes(r, tt):
-            words = xts[r][:].bitcast(F32)
-            tp = psum_tp.tile([P, 4, P], F32, name="tp", tag="tp")
-            for c in range(4):
-                col = tt * WORDS + (c // 2) * 2 * P + c % 2
-                nc.tensor.transpose(tp[:, c, :], words[:, col:col + 2 * P - 1:2], ident[:])
-            tps[r, tt] = tp
-            if tt == RT - 1 and r + NX < ROUNDS:
-                load(r + NX)
-
-        def copy_out(r, tt):
-            if tt == 0:
-                grouped = gpool.tile([P, RT * DIM], BF16, name="grouped", tag="grouped", align_bytes=64)
-                groupeds[r] = grouped
-            nc.scalar.copy(
-                out=groupeds[r][:].bitcast(F32)[:, tt * WORDS:(tt + 1) * WORDS].rearrange("p (g r u) -> p g r u", g=2, u=2),
-                in_=tps[r, tt][:].rearrange("p (g u) r -> p g r u", u=2),
-            )
-
-        def quantise(r, cuts):
-            xc = cpool.tile([P, RT * 2 * P], U32, name="xc", tag="xc", align_bytes=64)
-            xs = cpool.tile([P, RT * 2 * P], U8, name="xs", tag="xs", align_bytes=64)
-            codes[r], planes[r] = xc, xs
-            width = RT * 2 * P // cuts
-
-            def part(c):
-                nc.vector.quantize_mx(
-                    out=xc[:, c * width:(c + 1) * width].bitcast(FP8X4),
-                    scales=xs[:, c * width:(c + 1) * width],
-                    in_=groupeds[r][:, 4 * c * width:4 * (c + 1) * width],
-                )
-
-            return part
-
-        def project(r):
-            xc, xs = codes[r], planes[r]
-            qk = []
-            for half in range(2):
-                qkb = psum_qk.tile([P, BANK], F32, name="qkb", tag="qkb")
-                qk.append(qkb)
-            vb = psum_v.tile([P, BANK], F32, name="vb", tag="vb")
-            for tt in range(RT):
-                for g in range(2):
-                    sl = slice((tt * 2 + g) * P, (tt * 2 + g + 1) * P)
-                    nc.tensor.matmul_mx(
-                        out=qk[tt // 2][:, (tt % 2) * QK:(tt % 2 + 1) * QK],
-                        lhsT=xc[:, sl].bitcast(FP8X4), lhsT_scale=xs[:, sl],
-                        rhs=wc_qk[:, g * QK:(g + 1) * QK].bitcast(FP8X4), rhs_scale=ws_qk[:, g * QK:(g + 1) * QK],
-                        start=(g == 0), stop=(g == 1),
-                    )
-                    nc.tensor.matmul_mx(
-                        out=vb[:, tt * P:(tt + 1) * P],
-                        lhsT=xc[:, sl].bitcast(FP8X4), lhsT_scale=xs[:, sl],
-                        rhs=wc_v[:, g * P:(g + 1) * P].bitcast(FP8X4), rhs_scale=ws_v[:, g * P:(g + 1) * P],
-                        start=(g == 0), stop=(g == 1),
-                    )
-            qkbanks[r], vbanks[r] = qk, vb
-
-        def stored_with(r):
-            return (r, 1) if r >= ROUNDS - 2 else (r - r % 2, 2)
-
-        def stage_tile(kind, r, rows):
-            first, count = stored_with(r)
-            if (kind, first) not in stages:
-                st = stage.tile([P, rows, 2 * RT, D], F32, name=kind, tag=kind)
-                stages[kind, first] = st
-            return stages[kind, first], (r - first) * RT
-
-        def store(dst, kind, r, row):
-            first, count = stored_with(r)
-            if r != first + count - 1:
-                return
-            b, j = divmod(first, RPB)
-            view = dst[b].rearrange("h (p t) d -> p h (t d)", t=TPB)
-            nt = count * RT
-            nc.sync.dma_start(
-                out=view[:, :, j * RT * D:(j * RT + nt) * D],
-                in_=stages[kind, first][:, row:row + H, 0:nt, :].rearrange("p h t d -> p h (t d)"),
-            )
-
-        def add_bias(r):
-            y = ypool.tile([P, RT, QK], F32, name="y", tag="y")
-            for half in range(2):
-                nc.vector.tensor_tensor(
-                    out=y[:, 2 * half:2 * half + 2, :],
-                    in0=qkbanks[r][half][:].rearrange("p (t c) -> p t c", t=2),
-                    in1=bias_qk[:].unsqueeze(1).to_broadcast([P, 2, QK]),
-                    op=ALU.add,
-                )
-            ys[r] = y
-            vst, tl = stage_tile("vst", r, H)
-            nc.vector.tensor_tensor(
-                out=vst[:, :, tl:tl + RT, :].rearrange("p h t d -> p t h d"),
-                in0=vbanks[r][:].rearrange("p (t h d) -> p t h d", t=RT, h=H),
-                in1=cv[:, 0:P].rearrange("p (h d) -> p h d", h=H).unsqueeze(1).to_broadcast([P, RT, H, D]),
-                op=ALU.add,
-            )
-            store(out_2, "vst", r, 0)
-
-        def squares(r):
-            ss = small.tile([P, GROUPS], F32, name="ss", tag="ss")
-            sq = jpool.tile([P, GROUPS, D], F32, name="sq", tag="sq")
-            for n in range(GROUPS):
-                nc.scalar.activation(
-                    out=sq[:, n, :], in_=ys[r][:, n // 4, (n % 4) * D:(n % 4 + 1) * D],
-                    func=ACT.Square, accum_out=ss[:, n:n + 1],
-                )
-            rr = small.tile([P, GROUPS], F32, name="rr", tag="rr")
-            nc.scalar.activation(out=rr[:], in_=ss[:], func=ACT.Abs_reciprocal_sqrt, scale=1.0 / D, bias=eps[:])
-            rrs[r] = rr
-
-        def products(r, half):
-            if half == 0:
-                pr = ppool.tile([P, GROUPS, 2, D], F32, name="pr", tag="pr")
-                prods[r] = pr
-            shape = [P, 2 * HALF, H, D, 2]
-            nc.vector.tensor_tensor(
-                out=prods[r][:, half * GROUPS // 2:(half + 1) * GROUPS // 2].rearrange("p (m h) b (i a) -> p m h (b i) a", h=H, a=2),
-                in0=ys[r][:, half * HALF:(half + 1) * HALF, :].rearrange("p t (s h c) -> p (t s) h c", s=2, h=H).unsqueeze(4).to_broadcast(shape),
-                in1=tabs[r, half][:].rearrange("p t (s c a) -> p (t s) c a", s=2, a=2).unsqueeze(2).to_broadcast(shape),
-                op=ALU.mult,
-            )
-
-        def pair_add(r, half):
-            if half == 0:
-                sm = spool.tile([P, GROUPS, D], F32, name="sm", tag="sm")
-                sums[r] = sm
-            first, last = half * GROUPS // 2, (half + 1) * GROUPS // 2
-            if r == ROUNDS - 1 and half == 1:
-                mid = (first + last) // 2
-                nc.vector.tensor_tensor(
-                    out=sums[r][:, mid:last, :], in0=prods[r][:, mid:last, 0, :], in1=prods[r][:, mid:last, 1, :], op=ALU.add,
-                )
-                last = mid
-            nc.gpsimd.tensor_tensor(
-                out=sums[r][:, first:last, :], in0=prods[r][:, first:last, 0, :], in1=prods[r][:, first:last, 1, :], op=ALU.add,
-            )
-
-        def scale_out(r, half):
-            st, tl = stage_tile("qkst", r, 2 * H)
-            if half == 1 and r < ROUNDS - 1:
-                nc.gpsimd.tensor_tensor(
-                    out=st[:, :, tl + HALF:tl + RT, :].rearrange("p m t d -> p t m d"),
-                    in0=sums[r][:, GROUPS // 2:, :].rearrange("p (t m) d -> p t m d", t=HALF),
-                    in1=rrs[r][:, GROUPS // 2:].rearrange("p (t m) -> p t m", t=HALF).unsqueeze(3).to_broadcast([P, HALF, 2 * H, D]),
-                    op=ALU.mult,
-                )
-            else:
-                for n in range(half * GROUPS // 2, (half + 1) * GROUPS // 2):
-                    tt, m = divmod(n, 2 * H)
-                    if r == ROUNDS - 1 and n % 2 == 1:
-                        nc.vector.tensor_scalar(
-                            out=st[:, m, tl + tt, :], in0=sums[r][:, n, :], scalar1=rrs[r][:, n:n + 1], scalar2=None, op0=ALU.mult,
-                        )
-                    else:
-                        nc.scalar.activation(out=st[:, m, tl + tt, :], in_=sums[r][:, n, :], func=ACT.Copy, scale=rrs[r][:, n:n + 1])
-            if half == 1:
-                store(out_0, "qkst", r, 0)
-                store(out_1, "qkst", r, H)
-
-        def live(r):
-            return 0 <= r < ROUNDS
-
-        def transpose_round(r):
-            for tt in range(RT):
-                if tt >= TP_BANKS:
-                    copy_out(r, tt - TP_BANKS)
-                transposes(r, tt)
-            for tt in range(RT - TP_BANKS, RT):
-                copy_out(r, tt)
-
-        transpose_round(0)
-        part = quantise(0, 2)
-        part(0)
-        part(1)
-        transpose_round(1)
+        transposes(1)
+        copy_out(1)
         project(0)
         transpose_pe(0)
-        for tt in range(TP_BANKS):
-            transposes(2, tt)
-        for i in range(0, ROUNDS + 2):
+        transposes(2)
+        for i in range(0, CHUNKS + 2):
             if live(i + 2):
-                copy_out(i + 2, 0)
-                transposes(i + 2, RT - 1)
-                for tt in range(1, RT - 1):
-                    copy_out(i + 2, tt)
-            if i == 0:
-                add_bias(0)
+                copy_out(i + 2)
             if live(i + 1):
-                quantise(i + 1, 1)(0)
+                quantise(i + 1)
                 project(i + 1)
-            if live(i) and i > 0:
-                add_bias(i)
-            if live(i - 2):
-                pair_add(i - 2, 0)
-                pair_add(i - 2, 1)
             if live(i):
+                add_bias(i)
                 squares(i)
+                table(i)
             if live(i - 2):
-                scale_out(i - 2, 0)
-                scale_out(i - 2, 1)
-            if live(i + 2):
-                copy_out(i + 2, RT - 1)
-            if 1 <= i + 1 < RPB:
-                transpose_pe(i + 1)
+                pair_add(i - 2)
+                scale_out(i - 2)
+            if i in (0, 2, 4):
+                transpose_pe(i // 2 + 1)
             if live(i + 3):
-                for tt in range(TP_BANKS):
-                    transposes(i + 3, tt)
-            for half in range(2):
-                if live(i - 1):
-                    products(i - 1, half)
-                if live(i):
-                    table(i, half)
+                transposes(i + 3)
+            if live(i - 1):
+                products(i - 1)

@@ -94,15 +94,14 @@ def tile_selfattention_pa_t_kernel(tc, x, pe, qkv_w, qkv_b, q_scale, k_scale, ou
         junk = const.tile([P, 1], F32, name="junk", tag="junk")
         nc.scalar.activation(out=junk[:], in_=eps[:], func=ACT.Abs_reciprocal_sqrt)
 
-        def transposes(h):
+        def transposes(h, tt):
             words = xts[h // LC][:].bitcast(F32)
-            for tt in range(CT):
-                tp = psum_tp.tile([P, 4, P], F32, name="tp", tag="tp")
-                for c in range(4):
-                    col = (h % LC * CT + tt) * WORDS + (c // 2) * 2 * P + c % 2
-                    nc.tensor.transpose(tp[:, c, :], words[:, col:col + 2 * P - 1:2], ident[:])
-                tps[h, tt] = tp
-            if h % LC == LC - 1 and h // LC + NX < CHUNKS // LC:
+            tp = psum_tp.tile([P, 4, P], F32, name="tp", tag="tp")
+            for c in range(4):
+                col = (h % LC * CT + tt) * WORDS + (c // 2) * 2 * P + c % 2
+                nc.tensor.transpose(tp[:, c, :], words[:, col:col + 2 * P - 1:2], ident[:])
+            tps[h, tt] = tp
+            if tt == CT - 1 and h % LC == LC - 1 and h // LC + NX < CHUNKS // LC:
                 load(h // LC + NX)
 
         def copy_out(h):
@@ -120,21 +119,21 @@ def tile_selfattention_pa_t_kernel(tc, x, pe, qkv_w, qkv_b, q_scale, k_scale, ou
             nc.vector.quantize_mx(out=xc[:].bitcast(FP8X4), scales=xs[:], in_=groupeds[h][:])
             codes[h] = xc, xs
 
-        def project(h):
+        def project(h, tt):
             xc, xs = codes[h]
-            qkb = psum_qk.tile([P, CT * QK], F32, name="qkb", tag="qkb")
-            vb = psum_v.tile([P, CT * P], F32, name="vb", tag="vb")
-            for bank, width, wc, ws in ((qkb, QK, wc_qk, ws_qk), (vb, P, wc_v, ws_v)):
-                for tt in range(CT):
-                    for g in range(2):
-                        sl = slice((tt * 2 + g) * P, (tt * 2 + g + 1) * P)
-                        nc.tensor.matmul_mx(
-                            out=bank[:, tt * width:(tt + 1) * width],
-                            lhsT=xc[:, sl].bitcast(FP8X4), lhsT_scale=xs[:, sl],
-                            rhs=wc[:, g * width:(g + 1) * width].bitcast(FP8X4), rhs_scale=ws[:, g * width:(g + 1) * width],
-                            start=(g == 0), stop=(g == 1),
-                        )
-            qkbanks[h], vbanks[h] = qkb, vb
+            if tt == 0:
+                qkb = psum_qk.tile([P, CT * QK], F32, name="qkb", tag="qkb")
+                vb = psum_v.tile([P, CT * P], F32, name="vb", tag="vb")
+                qkbanks[h], vbanks[h] = qkb, vb
+            for bank, width, wc, ws in ((qkbanks[h], QK, wc_qk, ws_qk), (vbanks[h], P, wc_v, ws_v)):
+                for g in range(2):
+                    sl = slice((tt * 2 + g) * P, (tt * 2 + g + 1) * P)
+                    nc.tensor.matmul_mx(
+                        out=bank[:, tt * width:(tt + 1) * width],
+                        lhsT=xc[:, sl].bitcast(FP8X4), lhsT_scale=xs[:, sl],
+                        rhs=wc[:, g * width:(g + 1) * width].bitcast(FP8X4), rhs_scale=ws[:, g * width:(g + 1) * width],
+                        start=(g == 0), stop=(g == 1),
+                    )
 
         def stored_with(h):
             if h >= CHUNKS - 2:
@@ -192,12 +191,12 @@ def tile_selfattention_pa_t_kernel(tc, x, pe, qkv_w, qkv_b, q_scale, k_scale, ou
             nc.scalar.activation(out=rr[:], in_=ss[:], func=ACT.Abs_reciprocal_sqrt, scale=1.0 / D, bias=eps[:])
             rrs[h] = rr
 
-        def table(h):
-            tab = psum_tab.tile([P, CT, 2 * P], F32, name="tab", tag="tab")
-            for tt in range(CT):
-                t = h % CPB * CT + tt
-                nc.tensor.matmul(out=tab[:, tt, :], lhsT=pe_t[:, t, :], rhs=diag[:], start=True, stop=True)
-            tabs[h] = tab
+        def table(h, tt):
+            if tt == 0:
+                tab = psum_tab.tile([P, CT, 2 * P], F32, name="tab", tag="tab")
+                tabs[h] = tab
+            t = h % CPB * CT + tt
+            nc.tensor.matmul(out=tabs[h][:, tt, :], lhsT=pe_t[:, t, :], rhs=diag[:], start=True, stop=True)
 
         def products(h):
             pr = ppool.tile([P, GROUPS, 2, D], F32, name="pr", tag="pr")
@@ -239,7 +238,8 @@ def tile_selfattention_pa_t_kernel(tc, x, pe, qkv_w, qkv_b, q_scale, k_scale, ou
             store(out_0, "qkst", h, 0)
             store(out_1, "qkst", h, H)
 
-        transposes(0)
+        for tt in range(CT):
+            transposes(0, tt)
         copy_out(0)
         wg_qk = const.tile([P, 2, QK, 4], BF16, name="wg_qk", tag="wg_qk", align_bytes=64)
         wg_v = const.tile([P, 2, P, 4], BF16, name="wg_v", tag="wg_v", align_bytes=64)
@@ -288,27 +288,33 @@ def tile_selfattention_pa_t_kernel(tc, x, pe, qkv_w, qkv_b, q_scale, k_scale, ou
         def live(h):
             return 0 <= h < CHUNKS
 
-        transposes(1)
+        for tt in range(CT):
+            transposes(1, tt)
         copy_out(1)
-        project(0)
+        for tt in range(CT):
+            project(0, tt)
         transpose_pe(0)
-        transposes(2)
+        for tt in range(CT):
+            transposes(2, tt)
         for i in range(0, CHUNKS + 2):
             if live(i + 2):
                 copy_out(i + 2)
             if live(i + 1):
                 quantise(i + 1)
-                project(i + 1)
+            if i in (0, 2, 4):
+                transpose_pe(i // 2 + 1)
+            for tt in range(CT):
+                if live(i + 1):
+                    project(i + 1, tt)
+                if live(i):
+                    table(i, tt)
+                if live(i + 3):
+                    transposes(i + 3, tt)
             if live(i):
                 add_bias(i)
                 squares(i)
-                table(i)
             if live(i - 2):
                 pair_add(i - 2)
                 scale_out(i - 2)
-            if i in (0, 2, 4):
-                transpose_pe(i // 2 + 1)
-            if live(i + 3):
-                transposes(i + 3)
             if live(i - 1):
                 products(i - 1)

@@ -203,8 +203,8 @@ def tile_selfattention_pa_t_kernel(tc, x, pe, qkv_w, qkv_b, q_scale, k_scale, ou
             shape = [P, CT * 2, H, D, 2]
             nc.vector.tensor_tensor(
                 out=pr[:].rearrange("p (m h) b (i a) -> p m h (b i) a", h=H, a=2),
-                in0=ys[h][:].rearrange("p t (s h c) -> p (t s) h c", s=2, h=H).unsqueeze(4).to_broadcast(shape),
-                in1=tabs[h][:].rearrange("p t (s c a) -> p (t s) c a", s=2, a=2).unsqueeze(2).to_broadcast(shape),
+                in0=tabs[h][:].rearrange("p t (s c a) -> p (t s) c a", s=2, a=2).unsqueeze(2).to_broadcast(shape),
+                in1=ys[h][:].rearrange("p t (s h c) -> p (t s) h c", s=2, h=H).unsqueeze(4).to_broadcast(shape),
                 op=ALU.mult,
             )
             prods[h] = pr

@@ -16,15 +16,16 @@ EPS = 1e-6
 P = 128
 TPB = L // P
 CT = 2
-CPB = TPB // CT
-CHUNKS = B * CPB
+CPR = 2
+RT = CPR * CT
+ROUNDS = B * TPB // RT
+CHUNKS = ROUNDS * CPR
 ROWS = 2 * H
 GROUPS = CT * ROWS
 QK = ROWS * D
 PAIRS = D // 2
 WORDS = DIM // 2
 BANK = 512
-LC = 2
 NX = 6
 SCALAR_GROUPS = 6
 FLOPS = 2 * B * L * DIM * 3 * H * D
@@ -52,15 +53,15 @@ def tile_selfattention_pa_t_kernel(tc, x, pe, qkv_w, qkv_b, q_scale, k_scale, ou
         xts, tps, groupeds, codes = {}, {}, {}, {}
         qkbanks, vbanks, ys, tabs, prods, sums, rrs, stages = {}, {}, {}, {}, {}, {}, {}, {}
 
-        def load(m, cuts=1, part=0):
-            b, j = divmod(m, CPB // LC)
+        def load(r, cuts=1, part=0):
+            j, b = divmod(r, B)
             if part == 0:
-                xt = xpool.tile([P, LC * CT * DIM], BF16, name="xt", tag="xt")
-                xts[m] = xt
+                xt = xpool.tile([P, RT * DIM], BF16, name="xt", tag="xt")
+                xts[r] = xt
             src = x[b].rearrange("(p t) k -> p (t k)", t=TPB)
-            width = LC * CT * DIM // cuts
-            first = j * LC * CT * DIM + part * width
-            nc.sync.dma_start(out=xts[m][:, part * width:(part + 1) * width], in_=src[:, first:first + width])
+            width = RT * DIM // cuts
+            first = j * RT * DIM + part * width
+            nc.sync.dma_start(out=xts[r][:, part * width:(part + 1) * width], in_=src[:, first:first + width])
 
         load(0, 4, 0)
         load(0, 4, 1)
@@ -79,9 +80,9 @@ def tile_selfattention_pa_t_kernel(tc, x, pe, qkv_w, qkv_b, q_scale, k_scale, ou
         pe_src = pe[0, 0].rearrange("(p t) i a b -> p (t i a b)", t=TPB)
         nc.sync.dma_start(out=pe_sb[:, 0:4 * P], in_=pe_src[:, 0:4 * P])
         load(1)
+        for r in range(2, NX):
+            load(r)
         nc.sync.dma_start(out=pe_sb[:, 4 * P:], in_=pe_src[:, 4 * P:])
-        for m in range(2, NX):
-            load(m)
 
         ident = const.tile([P, P], F32, name="ident", tag="ident")
         make_identity(nc, ident[:])
@@ -95,14 +96,16 @@ def tile_selfattention_pa_t_kernel(tc, x, pe, qkv_w, qkv_b, q_scale, k_scale, ou
         nc.scalar.activation(out=junk[:], in_=eps[:], func=ACT.Abs_reciprocal_sqrt)
 
         def transposes(h, tt):
-            words = xts[h // LC][:].bitcast(F32)
+            words = xts[h // CPR][:].bitcast(F32)
             tp = psum_tp.tile([P, 4, P], F32, name="tp", tag="tp")
+            if tt > 0:
+                nc.tensor.matmul(out=tp[:, 0, :], lhsT=ident[:], rhs=ident[:], start=True, stop=True)
             for c in range(4):
-                col = (h % LC * CT + tt) * WORDS + (c // 2) * 2 * P + c % 2
+                col = (h % CPR * CT + tt) * WORDS + (c // 2) * 2 * P + c % 2
                 nc.tensor.transpose(tp[:, c, :], words[:, col:col + 2 * P - 1:2], ident[:])
             tps[h, tt] = tp
-            if tt == CT - 1 and h % LC == LC - 1 and h // LC + NX < CHUNKS // LC:
-                load(h // LC + NX)
+            if tt == CT - 1 and h % CPR == CPR - 1 and h // CPR + NX < ROUNDS:
+                load(h // CPR + NX)
 
         def copy_out(h):
             grouped = gpool.tile([P, CT * DIM], BF16, name="grouped", tag="grouped", align_bytes=64)
@@ -136,16 +139,12 @@ def tile_selfattention_pa_t_kernel(tc, x, pe, qkv_w, qkv_b, q_scale, k_scale, ou
                     )
 
         def stored_with(h):
-            if h >= CHUNKS - 2:
-                return h, 1
-            if h >= CHUNKS - 4:
-                return CHUNKS - 4, 2
-            return h - h % 4, 4
+            return (h, 1) if h >= CHUNKS - CPR else (h - h % CPR, CPR)
 
         def stage_tile(kind, h, rows):
             first, count = stored_with(h)
             if (kind, first) not in stages:
-                st = stage.tile([P, rows, 4 * CT, D], F32, name=kind, tag=kind)
+                st = stage.tile([P, rows, RT, D], F32, name=kind, tag=kind)
                 stages[kind, first] = st
             return stages[kind, first], (h - first) * CT
 
@@ -153,11 +152,11 @@ def tile_selfattention_pa_t_kernel(tc, x, pe, qkv_w, qkv_b, q_scale, k_scale, ou
             first, count = stored_with(h)
             if h != first + count - 1:
                 return
-            b, j = divmod(first, CPB)
+            j, b = divmod(first // CPR, B)
             view = dst[b].rearrange("h (p t) d -> p h (t d)", t=TPB)
-            nt = count * CT
+            t, nt = j * RT + first % CPR * CT, count * CT
             nc.sync.dma_start(
-                out=view[:, :, j * CT * D:(j * CT + nt) * D],
+                out=view[:, :, t * D:(t + nt) * D],
                 in_=stages[kind, first][:, row:row + H, 0:nt, :].rearrange("p h t d -> p h (t d)"),
             )
 
@@ -191,19 +190,22 @@ def tile_selfattention_pa_t_kernel(tc, x, pe, qkv_w, qkv_b, q_scale, k_scale, ou
             nc.scalar.activation(out=rr[:], in_=ss[:], func=ACT.Abs_reciprocal_sqrt, scale=1.0 / D, bias=eps[:])
             rrs[h] = rr
 
-        def table(h, tt):
-            if tt == 0:
-                tab = psum_tab.tile([P, CT, 2 * P], F32, name="tab", tag="tab")
-                tabs[h] = tab
-            t = h % CPB * CT + tt
-            nc.tensor.matmul(out=tabs[h][:, tt, :], lhsT=pe_t[:, t, :], rhs=diag[:], start=True, stop=True)
+        def place(h):
+            return h // CPR // B, h % CPR
+
+        def table(h):
+            tab = psum_tab.tile([P, CT, 2 * P], F32, name="tab", tag="tab")
+            j, c = place(h)
+            for tt in range(CT):
+                nc.tensor.matmul(out=tab[:, tt, :], lhsT=pe_t[:, j * RT + c * CT + tt, :], rhs=diag[:], start=True, stop=True)
+            tabs[j, c] = tab
 
         def products(h):
             pr = ppool.tile([P, GROUPS, 2, D], F32, name="pr", tag="pr")
             shape = [P, CT * 2, H, D, 2]
             nc.vector.tensor_tensor(
                 out=pr[:].rearrange("p (m h) b (i a) -> p m h (b i) a", h=H, a=2),
-                in0=tabs[h][:].rearrange("p t (s c a) -> p (t s) c a", s=2, a=2).unsqueeze(2).to_broadcast(shape),
+                in0=tabs[place(h)][:].rearrange("p t (s c a) -> p (t s) c a", s=2, a=2).unsqueeze(2).to_broadcast(shape),
                 in1=ys[h][:].rearrange("p t (s h c) -> p (t s) h c", s=2, h=H).unsqueeze(4).to_broadcast(shape),
                 op=ALU.mult,
             )
@@ -301,14 +303,15 @@ def tile_selfattention_pa_t_kernel(tc, x, pe, qkv_w, qkv_b, q_scale, k_scale, ou
                 copy_out(i + 2)
             if live(i + 1):
                 quantise(i + 1)
-            if i in (0, 2, 4):
-                transpose_pe(i // 2 + 1)
-            for tt in range(CT):
-                if live(i + 1):
+            if i in (4, 12, 20):
+                transpose_pe((i + 4) // 8)
+            if live(i + 1):
+                for tt in range(CT):
                     project(i + 1, tt)
-                if live(i):
-                    table(i, tt)
-                if live(i + 3):
+            if live(i) and i // CPR % B == 0:
+                table(i)
+            if live(i + 3):
+                for tt in range(CT):
                     transposes(i + 3, tt)
             if live(i):
                 add_bias(i)

@@ -15,19 +15,19 @@ B, L, DIM, H, D = 4, 2048, 1024, 2, 64
 EPS = 1e-6
 P = 128
 TPB = L // P
-CT = 2
-CPR = 2
-RT = CPR * CT
+RT = 4
+HALF = RT // 2
 ROUNDS = B * TPB // RT
-CHUNKS = ROUNDS * CPR
+TILES = ROUNDS * RT
 ROWS = 2 * H
-GROUPS = CT * ROWS
+GROUPS = RT * ROWS
 QK = ROWS * D
 PAIRS = D // 2
 WORDS = DIM // 2
 BANK = 512
 NX = 6
-SCALAR_GROUPS = 6
+TP_BANKS = 3
+SCALAR_GROUPS = GROUPS - ROWS
 FLOPS = 2 * B * L * DIM * 3 * H * D
 
 
@@ -37,19 +37,20 @@ def tile_selfattention_pa_t_kernel(tc, x, pe, qkv_w, qkv_b, q_scale, k_scale, ou
         const = ctx.enter_context(tc.tile_pool(name="const", bufs=1))
         xpool = ctx.enter_context(tc.tile_pool(name="xpool", bufs=NX))
         gpool = ctx.enter_context(tc.tile_pool(name="gpool", bufs=3))
-        cpool = ctx.enter_context(tc.tile_pool(name="cpool", bufs=3))
-        ypool = ctx.enter_context(tc.tile_pool(name="ypool", bufs=3))
-        ppool = ctx.enter_context(tc.tile_pool(name="ppool", bufs=3))
-        spool = ctx.enter_context(tc.tile_pool(name="spool", bufs=3))
-        jpool = ctx.enter_context(tc.tile_pool(name="jpool", bufs=2))
+        cpool = ctx.enter_context(tc.tile_pool(name="cpool", bufs=2))
+        ypool = ctx.enter_context(tc.tile_pool(name="ypool", bufs=2))
+        ppool = ctx.enter_context(tc.tile_pool(name="ppool", bufs=2))
+        spool = ctx.enter_context(tc.tile_pool(name="spool", bufs=2))
+        jpool = ctx.enter_context(tc.tile_pool(name="jpool", bufs=1))
         small = ctx.enter_context(tc.tile_pool(name="small", bufs=4))
         stage = ctx.enter_context(tc.tile_pool(name="stage", bufs=3))
-        psum_tp = ctx.enter_context(tc.psum_pool(name="psum_tp", bufs=2))
+        psum_tp = ctx.enter_context(tc.psum_pool(name="psum_tp", bufs=TP_BANKS))
         psum_qk = ctx.enter_context(tc.psum_pool(name="psum_qk", bufs=2))
-        psum_v = ctx.enter_context(tc.psum_pool(name="psum_v", bufs=2))
+        psum_v = ctx.enter_context(tc.psum_pool(name="psum_v", bufs=1))
         psum_tab = ctx.enter_context(tc.psum_pool(name="psum_tab", bufs=2))
         ctx.enter_context(tc.manual_schedule())
 
+        banks, copied = [], set()
         xts, tps, groupeds, codes = {}, {}, {}, {}
         qkbanks, vbanks, ys, tabs, prods, sums, rrs, stages = {}, {}, {}, {}, {}, {}, {}, {}
 
@@ -75,7 +76,8 @@ def tile_selfattention_pa_t_kernel(tc, x, pe, qkv_w, qkv_b, q_scale, k_scale, ou
         nc.sync.dma_start(out=row[0:1, 0:3 * P], in_=qkv_b.unsqueeze(0))
         nc.sync.dma_start(out=row[0:1, 3 * P:3 * P + D], in_=q_scale.unsqueeze(0))
         nc.sync.dma_start(out=row[0:1, 3 * P + D:BANK], in_=k_scale.unsqueeze(0))
-        load(0, 2, 1)
+        load(0, 4, 2)
+        load(0, 4, 3)
         pe_sb = const.tile([P, TPB * P], BF16, name="pe_sb", tag="pe_sb")
         pe_src = pe[0, 0].rearrange("(p t) i a b -> p (t i a b)", t=TPB)
         nc.sync.dma_start(out=pe_sb[:, 0:4 * P], in_=pe_src[:, 0:4 * P])
@@ -95,229 +97,283 @@ def tile_selfattention_pa_t_kernel(tc, x, pe, qkv_w, qkv_b, q_scale, k_scale, ou
         junk = const.tile([P, 1], F32, name="junk", tag="junk")
         nc.scalar.activation(out=junk[:], in_=eps[:], func=ACT.Abs_reciprocal_sqrt)
 
-        def transposes(h, tt):
-            words = xts[h // CPR][:].bitcast(F32)
+        def transposes(u):
+            r, tt = divmod(u, RT)
+            words = xts[r][:].bitcast(F32)
             tp = psum_tp.tile([P, 4, P], F32, name="tp", tag="tp")
-            if tt > 0:
-                nc.tensor.matmul(out=tp[:, 0, :], lhsT=ident[:], rhs=ident[:], start=True, stop=True)
             for c in range(4):
-                col = (h % CPR * CT + tt) * WORDS + (c // 2) * 2 * P + c % 2
+                col = tt * WORDS + (c // 2) * 2 * P + c % 2
                 nc.tensor.transpose(tp[:, c, :], words[:, col:col + 2 * P - 1:2], ident[:])
-            tps[h, tt] = tp
-            if tt == CT - 1 and h % CPR == CPR - 1 and h // CPR + NX < ROUNDS:
-                load(h // CPR + NX)
+            tps[u] = tp
+            banks.append(u)
+            if tt == RT - 1 and r + NX < ROUNDS:
+                load(r + NX)
 
-        def copy_out(h):
-            grouped = gpool.tile([P, CT * DIM], BF16, name="grouped", tag="grouped", align_bytes=64)
-            groupeds[h] = grouped
-            for tt in range(CT):
-                nc.scalar.copy(
-                    out=grouped[:].bitcast(F32)[:, tt * WORDS:(tt + 1) * WORDS].rearrange("p (g r u) -> p g r u", g=2, u=2),
-                    in_=tps[h, tt][:].rearrange("p (g u) r -> p g r u", u=2),
+        def copy_out(u):
+            r, tt = divmod(u, RT)
+            if tt == 0:
+                grouped = gpool.tile([P, RT * DIM], BF16, name="grouped", tag="grouped", align_bytes=64)
+                groupeds[r] = grouped
+            nc.scalar.copy(
+                out=groupeds[r][:].bitcast(F32)[:, tt * WORDS:(tt + 1) * WORDS].rearrange("p (g r v) -> p g r v", g=2, v=2),
+                in_=tps[u][:].rearrange("p (g v) r -> p g r v", v=2),
+            )
+            copied.add(u)
+
+        def fill_banks(most=TP_BANKS):
+            for n in range(most):
+                u = len(tps)
+                if u < TILES and (len(banks) < TP_BANKS or banks[-TP_BANKS] in copied):
+                    transposes(u)
+
+        def quantise(r, cuts=1):
+            xc = cpool.tile([P, RT * 2 * P], U32, name="xc", tag="xc", align_bytes=64)
+            xs = cpool.tile([P, RT * 2 * P], U8, name="xs", tag="xs", align_bytes=64)
+            codes[r] = xc, xs
+            width = RT * 2 * P // cuts
+
+            def part(c):
+                nc.vector.quantize_mx(
+                    out=xc[:, c * width:(c + 1) * width].bitcast(FP8X4),
+                    scales=xs[:, c * width:(c + 1) * width],
+                    in_=groupeds[r][:, 4 * c * width:4 * (c + 1) * width],
                 )
 
-        def quantise(h):
-            xc = cpool.tile([P, CT * 2 * P], U32, name="xc", tag="xc", align_bytes=64)
-            xs = cpool.tile([P, CT * 2 * P], U8, name="xs", tag="xs", align_bytes=64)
-            nc.vector.quantize_mx(out=xc[:].bitcast(FP8X4), scales=xs[:], in_=groupeds[h][:])
-            codes[h] = xc, xs
+            return part
 
-        def project(h, tt):
-            xc, xs = codes[h]
-            if tt == 0:
-                qkb = psum_qk.tile([P, CT * QK], F32, name="qkb", tag="qkb")
-                vb = psum_v.tile([P, CT * P], F32, name="vb", tag="vb")
-                qkbanks[h], vbanks[h] = qkb, vb
-            for bank, width, wc, ws in ((qkbanks[h], QK, wc_qk, ws_qk), (vbanks[h], P, wc_v, ws_v)):
+        def project(r, tiles, bank, width, wc, ws):
+            xc, xs = codes[r]
+            for n, tt in enumerate(tiles):
                 for g in range(2):
                     sl = slice((tt * 2 + g) * P, (tt * 2 + g + 1) * P)
                     nc.tensor.matmul_mx(
-                        out=bank[:, tt * width:(tt + 1) * width],
+                        out=bank[:, n * width:(n + 1) * width],
                         lhsT=xc[:, sl].bitcast(FP8X4), lhsT_scale=xs[:, sl],
                         rhs=wc[:, g * width:(g + 1) * width].bitcast(FP8X4), rhs_scale=ws[:, g * width:(g + 1) * width],
                         start=(g == 0), stop=(g == 1),
                     )
 
-        def stored_with(h):
-            return (h, 1) if h >= CHUNKS - CPR else (h - h % CPR, CPR)
+        def project_qk(r, half):
+            qkb = psum_qk.tile([P, BANK], F32, name="qkb", tag="qkb")
+            qkbanks[r, half] = qkb
+            project(r, range(half * HALF, (half + 1) * HALF), qkb, QK, wc_qk, ws_qk)
 
-        def stage_tile(kind, h, rows):
-            first, count = stored_with(h)
-            if (kind, first) not in stages:
+        def project_v(r):
+            vb = psum_v.tile([P, BANK], F32, name="vb", tag="vb")
+            vbanks[r] = vb
+            project(r, range(RT), vb, P, wc_v, ws_v)
+
+        def stage_tile(kind, r, rows):
+            if (kind, r) not in stages:
                 st = stage.tile([P, rows, RT, D], F32, name=kind, tag=kind)
-                stages[kind, first] = st
-            return stages[kind, first], (h - first) * CT
+                stages[kind, r] = st
+            return stages[kind, r]
 
-        def store(dst, kind, h, row):
-            first, count = stored_with(h)
-            if h != first + count - 1:
-                return
-            j, b = divmod(first // CPR, B)
+        def store(dst, kind, r, row, first=0, last=RT):
+            j, b = divmod(r, B)
             view = dst[b].rearrange("h (p t) d -> p h (t d)", t=TPB)
-            t, nt = j * RT + first % CPR * CT, count * CT
             nc.sync.dma_start(
-                out=view[:, :, t * D:(t + nt) * D],
-                in_=stages[kind, first][:, row:row + H, 0:nt, :].rearrange("p h t d -> p h (t d)"),
+                out=view[:, :, (j * RT + first) * D:(j * RT + last) * D],
+                in_=stages[kind, r][:, row:row + H, first:last, :].rearrange("p h t d -> p h (t d)"),
             )
 
-        def add_bias(h):
-            y = ypool.tile([P, CT, QK], F32, name="y", tag="y")
+        def add_bias(r):
+            y = ypool.tile([P, RT, QK], F32, name="y", tag="y")
+            for half in range(2):
+                nc.vector.tensor_tensor(
+                    out=y[:, HALF * half:HALF * (half + 1), :],
+                    in0=qkbanks[r, half][:].rearrange("p (t c) -> p t c", t=HALF),
+                    in1=bias_qk[:].unsqueeze(1).to_broadcast([P, HALF, QK]),
+                    op=ALU.add,
+                )
+            ys[r] = y
+            vst = stage_tile("vst", r, H)
             nc.vector.tensor_tensor(
-                out=y[:],
-                in0=qkbanks[h][:].rearrange("p (t c) -> p t c", t=CT),
-                in1=bias_qk[:].unsqueeze(1).to_broadcast([P, CT, QK]),
+                out=vst[:].rearrange("p h t d -> p t h d"),
+                in0=vbanks[r][:].rearrange("p (t h d) -> p t h d", t=RT, h=H),
+                in1=cv[:, 0:P].rearrange("p (h d) -> p h d", h=H).unsqueeze(1).to_broadcast([P, RT, H, D]),
                 op=ALU.add,
             )
-            ys[h] = y
-            vst, tl = stage_tile("vst", h, H)
-            nc.vector.tensor_tensor(
-                out=vst[:, :, tl:tl + CT, :].rearrange("p h t d -> p t h d"),
-                in0=vbanks[h][:].rearrange("p (t h d) -> p t h d", t=CT, h=H),
-                in1=cv[:, 0:P].rearrange("p (h d) -> p h d", h=H).unsqueeze(1).to_broadcast([P, CT, H, D]),
-                op=ALU.add,
-            )
-            store(out_2, "vst", h, 0)
+            store(out_2, "vst", r, 0)
 
-        def squares(h):
+        def squares(r):
             ss = small.tile([P, GROUPS], F32, name="ss", tag="ss")
             sq = jpool.tile([P, GROUPS, D], F32, name="sq", tag="sq")
             for n in range(GROUPS):
                 tt, m = divmod(n, ROWS)
                 nc.scalar.activation(
-                    out=sq[:, n, :], in_=ys[h][:, tt, m * D:(m + 1) * D], func=ACT.Square, accum_out=ss[:, n:n + 1],
+                    out=sq[:, n, :], in_=ys[r][:, tt, m * D:(m + 1) * D], func=ACT.Square, accum_out=ss[:, n:n + 1],
                 )
             rr = small.tile([P, GROUPS], F32, name="rr", tag="rr")
             nc.scalar.activation(out=rr[:], in_=ss[:], func=ACT.Abs_reciprocal_sqrt, scale=1.0 / D, bias=eps[:])
-            rrs[h] = rr
+            rrs[r] = rr
 
-        def place(h):
-            return h // CPR // B, h % CPR
+        def table(j, half):
+            tab = psum_tab.tile([P, HALF, 2 * P], F32, name="tab", tag="tab")
+            for tt in range(HALF):
+                nc.tensor.matmul(out=tab[:, tt, :], lhsT=pe_t[:, j * RT + half * HALF + tt, :], rhs=diag[:], start=True, stop=True)
+            tabs[j, half] = tab
 
-        def table(h):
-            tab = psum_tab.tile([P, CT, 2 * P], F32, name="tab", tag="tab")
-            j, c = place(h)
-            for tt in range(CT):
-                nc.tensor.matmul(out=tab[:, tt, :], lhsT=pe_t[:, j * RT + c * CT + tt, :], rhs=diag[:], start=True, stop=True)
-            tabs[j, c] = tab
-
-        def products(h):
-            pr = ppool.tile([P, GROUPS, 2, D], F32, name="pr", tag="pr")
-            shape = [P, CT * 2, H, D, 2]
+        def products(r, half):
+            if half == 0:
+                pr = ppool.tile([P, GROUPS, 2, D], F32, name="pr", tag="pr")
+                prods[r] = pr
+            shape = [P, HALF * 2, H, D, 2]
             nc.vector.tensor_tensor(
-                out=pr[:].rearrange("p (m h) b (i a) -> p m h (b i) a", h=H, a=2),
-                in0=tabs[place(h)][:].rearrange("p t (s c a) -> p (t s) c a", s=2, a=2).unsqueeze(2).to_broadcast(shape),
-                in1=ys[h][:].rearrange("p t (s h c) -> p (t s) h c", s=2, h=H).unsqueeze(4).to_broadcast(shape),
+                out=prods[r][:, half * HALF * ROWS:(half + 1) * HALF * ROWS].rearrange("p (m h) b (i a) -> p m h (b i) a", h=H, a=2),
+                in0=tabs[r // B, half][:].rearrange("p t (s c a) -> p (t s) c a", s=2, a=2).unsqueeze(2).to_broadcast(shape),
+                in1=ys[r][:, half * HALF:(half + 1) * HALF, :].rearrange("p t (s h c) -> p (t s) h c", s=2, h=H).unsqueeze(4).to_broadcast(shape),
                 op=ALU.mult,
             )
-            prods[h] = pr
 
-        def pair_add(h):
-            sm = spool.tile([P, GROUPS, D], F32, name="sm", tag="sm")
-            sums[h] = sm
-            gn = GROUPS // 2 if h == CHUNKS - 1 else GROUPS
-            pr = prods[h]
-            if gn < GROUPS:
-                nc.vector.tensor_tensor(out=sm[:, gn:, :], in0=pr[:, gn:, 0, :], in1=pr[:, gn:, 1, :], op=ALU.add)
-            nc.gpsimd.tensor_tensor(out=sm[:, 0:gn, :], in0=pr[:, 0:gn, 0, :], in1=pr[:, 0:gn, 1, :], op=ALU.add)
+        def pair_add(r, first=0, last=GROUPS, eng=nc.gpsimd):
+            if first == 0:
+                sm = spool.tile([P, GROUPS, D], F32, name="sm", tag="sm")
+                sums[r] = sm
+            eng.tensor_tensor(
+                out=sums[r][:, first:last, :], in0=prods[r][:, first:last, 0, :], in1=prods[r][:, first:last, 1, :], op=ALU.add,
+            )
 
-        def scale_out(h):
-            st, tl = stage_tile("qkst", h, ROWS)
-            sm, rr = sums[h], rrs[h]
-            last = h == CHUNKS - 1
-            if not last:
+        def scale_by_scalar(r, count):
+            st = stage_tile("qkst", r, ROWS)
+            for n in range(count):
+                tt, m = divmod(n, ROWS)
+                nc.scalar.activation(out=st[:, m, tt, :], in_=sums[r][:, n, :], func=ACT.Copy, scale=rrs[r][:, n:n + 1])
+
+        def scale_rest(r, count, eng):
+            st = stage_tile("qkst", r, ROWS)
+            tiles = (GROUPS - count) // ROWS
+            eng.tensor_tensor(
+                out=st[:, :, RT - tiles:, :].rearrange("p m t d -> p t m d"),
+                in0=sums[r][:, count:, :].rearrange("p (t m) d -> p t m d", t=tiles),
+                in1=rrs[r][:, count:].rearrange("p (t m) -> p t m", t=tiles).unsqueeze(3).to_broadcast([P, tiles, ROWS, D]),
+                op=ALU.mult,
+            )
+
+        def store_qk(r, first=0, last=RT):
+            store(out_0, "qkst", r, 0, first, last)
+            store(out_1, "qkst", r, H, first, last)
+
+        def constants():
+            cps = psum_tab.tile([P, BANK], F32, name="cps", tag="tab")
+            nc.tensor.matmul(out=cps[:], lhsT=ones[:], rhs=row[:], start=True, stop=True)
+            nc.scalar.copy(
+                out=bias_qk[:].rearrange("p (n b i) -> p n b i", b=2, i=PAIRS),
+                in_=cps[:, 0:QK].rearrange("p (n i b) -> p n b i", i=PAIRS, b=2),
+            )
+            nc.scalar.copy(out=cv[:], in_=cps[:, QK:BANK])
+            for s in range(2):
                 nc.gpsimd.tensor_tensor(
-                    out=st[:, SCALAR_GROUPS - ROWS:, tl + 1, :],
-                    in0=sm[:, SCALAR_GROUPS:, :],
-                    in1=rr[:, SCALAR_GROUPS:].unsqueeze(2).to_broadcast([P, GROUPS - SCALAR_GROUPS, D]),
+                    out=diag[:, s * P:(s + 1) * P].rearrange("p (b i a) -> p b i a", b=2, a=2),
+                    in0=ident[:].rearrange("p (i a b) -> p b i a", a=2, b=2),
+                    in1=cv[:, P + s * D:P + (s + 1) * D].rearrange("p (i b) -> p b i", b=2).unsqueeze(3).to_broadcast([P, 2, PAIRS, 2]),
                     op=ALU.mult,
                 )
-            for n in range(GROUPS if last else SCALAR_GROUPS):
-                tt, m = divmod(n, ROWS)
-                if last and tt == 1:
-                    nc.vector.tensor_scalar(out=st[:, m, tl + tt, :], in0=sm[:, n, :], scalar1=rr[:, n:n + 1], scalar2=None, op0=ALU.mult)
-                else:
-                    nc.scalar.activation(out=st[:, m, tl + tt, :], in_=sm[:, n, :], func=ACT.Copy, scale=rr[:, n:n + 1])
-            store(out_0, "qkst", h, 0)
-            store(out_1, "qkst", h, H)
 
-        for tt in range(CT):
-            transposes(0, tt)
-        copy_out(0)
+        bias_qk = const.tile([P, QK], F32, name="bias_qk", tag="bias_qk")
+        cv = const.tile([P, QK], F32, name="cv", tag="cv")
+        diag = const.tile([P, 2 * P], BF16, name="diag", tag="diag")
+        pe_t = const.tile([P, TPB, P], BF16, name="pe_t", tag="pe_t")
+
+        def transpose_pe(j):
+            tp = psum_tp.tile([P, RT, P], BF16, name="tpe", tag="tp")
+            for t in range(RT):
+                nc.tensor.transpose(tp[:, t, :], pe_sb[:, (RT * j + t) * P:(RT * j + t + 1) * P], ident_bf[:])
+            nc.scalar.copy(out=pe_t[:, RT * j:RT * (j + 1), :], in_=tp[:])
+            banks.append(("pe", j))
+            copied.add(("pe", j))
+
         wg_qk = const.tile([P, 2, QK, 4], BF16, name="wg_qk", tag="wg_qk", align_bytes=64)
         wg_v = const.tile([P, 2, P, 4], BF16, name="wg_v", tag="wg_v", align_bytes=64)
-        for g in range(2):
-            for b in range(2):
-                nc.vector.tensor_copy(
-                    out=wg_qk[:, g].rearrange("p (n b i) t -> p n b i t", n=4, b=2)[:, :, b],
-                    in_=w_raw[:, 4 * g:4 * g + 4, 0:QK].rearrange("p t (n i b) -> p n i t b", i=PAIRS, b=2)[:, :, :, :, b],
-                )
-        for g in range(2):
-            nc.vector.tensor_copy(out=wg_v[:, g], in_=w_raw[:, 4 * g:4 * g + 4, QK:3 * P].rearrange("p t n -> p n t"))
         wc_qk = const.tile([P, 2 * QK], U32, name="wc_qk", tag="wc_qk", align_bytes=64)
         ws_qk = const.tile([P, 2 * QK], U8, name="ws_qk", tag="ws_qk", align_bytes=64)
         wc_v = const.tile([P, 2 * P], U32, name="wc_v", tag="wc_v", align_bytes=64)
         ws_v = const.tile([P, 2 * P], U8, name="ws_v", tag="ws_v", align_bytes=64)
-        nc.vector.quantize_mx(out=wc_qk[:].bitcast(FP8X4), scales=ws_qk[:], in_=wg_qk[:].rearrange("p g n t -> p (g n t)"))
-        quantise(0)
-        nc.vector.quantize_mx(out=wc_v[:].bitcast(FP8X4), scales=ws_v[:], in_=wg_v[:].rearrange("p g n t -> p (g n t)"))
 
-        cps = psum_tab.tile([P, BANK], F32, name="cps", tag="tab")
-        nc.tensor.matmul(out=cps[:], lhsT=ones[:], rhs=row[:], start=True, stop=True)
-        bias_qk = const.tile([P, QK], F32, name="bias_qk", tag="bias_qk")
-        nc.scalar.copy(
-            out=bias_qk[:].rearrange("p (n b i) -> p n b i", b=2, i=PAIRS),
-            in_=cps[:, 0:QK].rearrange("p (n i b) -> p n b i", i=PAIRS, b=2),
-        )
-        cv = const.tile([P, QK], F32, name="cv", tag="cv")
-        nc.scalar.copy(out=cv[:], in_=cps[:, QK:BANK])
+        def weights_qk():
+            for g in range(2):
+                for b in range(2):
+                    nc.vector.tensor_copy(
+                        out=wg_qk[:, g].rearrange("p (n b i) t -> p n b i t", n=4, b=2)[:, :, b],
+                        in_=w_raw[:, 4 * g:4 * g + 4, 0:QK].rearrange("p t (n i b) -> p n i t b", i=PAIRS, b=2)[:, :, :, :, b],
+                    )
+            nc.vector.quantize_mx(out=wc_qk[:].bitcast(FP8X4), scales=ws_qk[:], in_=wg_qk[:].rearrange("p g n t -> p (g n t)"))
 
-        diag = const.tile([P, 2 * P], BF16, name="diag", tag="diag")
-        for s in range(2):
-            nc.gpsimd.tensor_tensor(
-                out=diag[:, s * P:(s + 1) * P].rearrange("p (b i a) -> p b i a", b=2, a=2),
-                in0=ident[:].rearrange("p (i a b) -> p b i a", a=2, b=2),
-                in1=cv[:, P + s * D:P + (s + 1) * D].rearrange("p (i b) -> p b i", b=2).unsqueeze(3).to_broadcast([P, 2, PAIRS, 2]),
-                op=ALU.mult,
-            )
-        pe_t = const.tile([P, TPB, P], BF16, name="pe_t", tag="pe_t")
+        def weights_v():
+            for g in range(2):
+                nc.vector.tensor_copy(out=wg_v[:, g], in_=w_raw[:, 4 * g:4 * g + 4, QK:3 * P].rearrange("p t n -> p n t"))
+            nc.vector.quantize_mx(out=wc_v[:].bitcast(FP8X4), scales=ws_v[:], in_=wg_v[:].rearrange("p g n t -> p (g n t)"))
 
-        def transpose_pe(j):
-            tp = psum_tp.tile([P, 4, P], BF16, name="tpe", tag="tp")
-            for t in range(4):
-                nc.tensor.transpose(tp[:, t, :], pe_sb[:, (4 * j + t) * P:(4 * j + t + 1) * P], ident_bf[:])
-            nc.scalar.copy(out=pe_t[:, 4 * j:4 * j + 4, :], in_=tp[:])
+        def live(r):
+            return 0 <= r < ROUNDS
 
-        def live(h):
-            return 0 <= h < CHUNKS
-
-        for tt in range(CT):
-            transposes(1, tt)
+        fill_banks(2)
+        copy_out(0)
         copy_out(1)
-        for tt in range(CT):
-            project(0, tt)
+        constants()
+        fill_banks(2)
+        copy_out(2)
+        copy_out(3)
         transpose_pe(0)
-        for tt in range(CT):
-            transposes(2, tt)
-        for i in range(0, CHUNKS + 2):
-            if live(i + 2):
-                copy_out(i + 2)
-            if live(i + 1):
-                quantise(i + 1)
-            if i in (4, 12, 20):
-                transpose_pe((i + 4) // 8)
-            if live(i + 1):
-                for tt in range(CT):
-                    project(i + 1, tt)
-            if live(i) and i // CPR % B == 0:
-                table(i)
-            if live(i + 3):
-                for tt in range(CT):
-                    transposes(i + 3, tt)
-            if live(i):
-                add_bias(i)
-                squares(i)
+        weights_qk()
+        quantise_part = quantise(0, 2)
+        quantise_part(0)
+        project_qk(0, 0)
+        quantise_part(1)
+        project_qk(0, 1)
+        weights_v()
+        fill_banks(1)
+        project_v(0)
+        for half in range(2):
+            table(0, half)
+        fill_banks()
+        for u in range(4, 10):
+            copy_out(u)
+            fill_banks()
+        for i in range(ROUNDS):
+            u0 = 10 + i * RT
             if live(i - 2):
-                pair_add(i - 2)
-                scale_out(i - 2)
+                scale_by_scalar(i - 2, SCALAR_GROUPS)
+            for u in (u0, u0 + 1):
+                if u < TILES:
+                    copy_out(u)
+            if i == 0:
+                add_bias(0)
+                products(0, 0)
+                products(0, 1)
+            if live(i + 1):
+                quantise(i + 1)(0)
+            if i > 0:
+                add_bias(i)
+            if live(i + 1):
+                project_qk(i + 1, 0)
+                project_qk(i + 1, 1)
+                project_v(i + 1)
+            fill_banks()
+            if live(i - 2):
+                scale_rest(i - 2, SCALAR_GROUPS, nc.gpsimd)
+                store_qk(i - 2)
             if live(i - 1):
-                products(i - 1)
+                pair_add(i - 1)
+            squares(i)
+            for u in (u0 + 2, u0 + 3):
+                if u < TILES:
+                    copy_out(u)
+            for half in range(2):
+                if i > 0:
+                    products(i, half)
+                if i % B == B - 1 and live(i + 1):
+                    table((i + 1) // B, half)
+            if i + 1 < ROUNDS // B:
+                transpose_pe(i + 1)
+            fill_banks()
+        r = ROUNDS - 1
+        scale_by_scalar(r - 1, GROUPS // 2)
+        pair_add(r, 0, GROUPS // 2)
+        pair_add(r, GROUPS // 2, GROUPS, nc.vector)
+        scale_rest(r - 1, GROUPS // 2, nc.vector)
+        store_qk(r - 1)
+        scale_rest(r, GROUPS // 2, nc.vector)
+        store_qk(r, HALF, RT)
+        scale_by_scalar(r, GROUPS // 2)
+        store_qk(r, 0, HALF)

@@ -52,7 +52,7 @@ def tile_selfattention_pa_t_kernel(tc, x, pe, qkv_w, qkv_b, q_scale, k_scale, ou
 
         banks, copied = [], set()
         xts, tps, groupeds, codes = {}, {}, {}, {}
-        qkbanks, vbanks, ys, tabs, prods, sums, rrs, stages = {}, {}, {}, {}, {}, {}, {}, {}
+        qkbanks, vbanks, ys, tabs, prods, sums, sss, rrs, stages = {}, {}, {}, {}, {}, {}, {}, {}, {}
 
         def load(r, cuts=1, part=0):
             j, b = divmod(r, B)
@@ -204,8 +204,11 @@ def tile_selfattention_pa_t_kernel(tc, x, pe, qkv_w, qkv_b, q_scale, k_scale, ou
                 nc.scalar.activation(
                     out=sq[:, n, :], in_=ys[r][:, tt, m * D:(m + 1) * D], func=ACT.Square, accum_out=ss[:, n:n + 1],
                 )
+            sss[r] = ss
+
+        def norms(r):
             rr = small.tile([P, GROUPS], F32, name="rr", tag="rr")
-            nc.scalar.activation(out=rr[:], in_=ss[:], func=ACT.Abs_reciprocal_sqrt, scale=1.0 / D, bias=eps[:])
+            nc.scalar.activation(out=rr[:], in_=sss[r][:], func=ACT.Abs_reciprocal_sqrt, scale=1.0 / D, bias=eps[:])
             rrs[r] = rr
 
         def table(j, half):
@@ -226,10 +229,11 @@ def tile_selfattention_pa_t_kernel(tc, x, pe, qkv_w, qkv_b, q_scale, k_scale, ou
                 op=ALU.mult,
             )
 
-        def pair_add(r, first=0, last=GROUPS, eng=nc.gpsimd):
-            if first == 0:
-                sm = spool.tile([P, GROUPS, D], F32, name="sm", tag="sm")
-                sums[r] = sm
+        def sums_tile(r):
+            sm = spool.tile([P, GROUPS, D], F32, name="sm", tag="sm")
+            sums[r] = sm
+
+        def pair_add(r, first, last, eng):
             eng.tensor_tensor(
                 out=sums[r][:, first:last, :], in0=prods[r][:, first:last, 0, :], in1=prods[r][:, first:last, 1, :], op=ALU.add,
             )
@@ -240,10 +244,10 @@ def tile_selfattention_pa_t_kernel(tc, x, pe, qkv_w, qkv_b, q_scale, k_scale, ou
                 tt, m = divmod(n, ROWS)
                 nc.scalar.activation(out=st[:, m, tt, :], in_=sums[r][:, n, :], func=ACT.Copy, scale=rrs[r][:, n:n + 1])
 
-        def scale_rest(r, count, eng):
+        def scale_by_vector(r, count):
             st = stage_tile("qkst", r, ROWS)
             tiles = (GROUPS - count) // ROWS
-            eng.tensor_tensor(
+            nc.vector.tensor_tensor(
                 out=st[:, :, RT - tiles:, :].rearrange("p m t d -> p t m d"),
                 in0=sums[r][:, count:, :].rearrange("p (t m) d -> p t m d", t=tiles),
                 in1=rrs[r][:, count:].rearrange("p (t m) -> p t m", t=tiles).unsqueeze(3).to_broadcast([P, tiles, ROWS, D]),
@@ -319,6 +323,7 @@ def tile_selfattention_pa_t_kernel(tc, x, pe, qkv_w, qkv_b, q_scale, k_scale, ou
         quantise_part = quantise(0, 2)
         quantise_part(0)
         project_qk(0, 0)
+        fill_banks(2)
         quantise_part(1)
         project_qk(0, 1)
         weights_v()
@@ -343,6 +348,10 @@ def tile_selfattention_pa_t_kernel(tc, x, pe, qkv_w, qkv_b, q_scale, k_scale, ou
                 products(0, 1)
             if live(i + 1):
                 quantise(i + 1)(0)
+            if live(i - 1):
+                sums_tile(i - 1)
+                if live(i + 1):
+                    nc.vector.memset(sums[i - 1][:, 0, 0:1], 0.0)
             if i > 0:
                 add_bias(i)
             if live(i + 1):
@@ -350,30 +359,32 @@ def tile_selfattention_pa_t_kernel(tc, x, pe, qkv_w, qkv_b, q_scale, k_scale, ou
                 project_qk(i + 1, 1)
                 project_v(i + 1)
             fill_banks()
-            if live(i - 2):
-                scale_rest(i - 2, SCALAR_GROUPS, nc.gpsimd)
-                store_qk(i - 2)
             if live(i - 1):
-                pair_add(i - 1)
+                pair_add(i - 1, 0, GROUPS, nc.gpsimd)
             squares(i)
             for u in (u0 + 2, u0 + 3):
                 if u < TILES:
                     copy_out(u)
+                if u == u0 + 2:
+                    norms(i)
             for half in range(2):
                 if i > 0:
                     products(i, half)
                 if i % B == B - 1 and live(i + 1):
                     table((i + 1) // B, half)
+            if live(i - 2):
+                scale_by_vector(i - 2, SCALAR_GROUPS)
+                store_qk(i - 2)
             if i + 1 < ROUNDS // B:
                 transpose_pe(i + 1)
             fill_banks()
         r = ROUNDS - 1
-        scale_by_scalar(r - 1, GROUPS // 2)
-        pair_add(r, 0, GROUPS // 2)
-        pair_add(r, GROUPS // 2, GROUPS, nc.vector)
-        scale_rest(r - 1, GROUPS // 2, nc.vector)
+        scale_by_scalar(r - 1, GROUPS)
         store_qk(r - 1)
-        scale_rest(r, GROUPS // 2, nc.vector)
+        sums_tile(r)
+        pair_add(r, 0, ROWS, nc.gpsimd)
+        pair_add(r, ROWS, GROUPS, nc.vector)
+        scale_by_vector(r, GROUPS // 2)
         store_qk(r, HALF, RT)
         scale_by_scalar(r, GROUPS // 2)
         store_qk(r, 0, HALF)

from contextlib import ExitStack

import concourse.mybir as mybir
from concourse.masks import make_identity

F32 = mybir.dt.float32
BF16 = mybir.dt.bfloat16
U32 = mybir.dt.uint32
U8 = mybir.dt.uint8
FP8X4 = mybir.dt.float8_e4m3fn_x4
ALU = mybir.AluOpType
ACT = mybir.ActivationFunctionType

B, L, DIM, H, D = 4, 2048, 1024, 2, 64
EPS = 1e-6
P = 128
TPB = L // P
RT = 4
HALF = RT // 2
ROUNDS = B * TPB // RT
TILES = ROUNDS * RT
ROWS = 2 * H
GROUPS = RT * ROWS
QK = ROWS * D
PAIRS = D // 2
WORDS = DIM // 2
BANK = 512
NX = 6
TP_BANKS = 3
SCALAR_GROUPS = GROUPS - ROWS
FLOPS = 2 * B * L * DIM * 3 * H * D


def tile_selfattention_pa_t_kernel(tc, x, pe, qkv_w, qkv_b, q_scale, k_scale, out_0, out_1, out_2):
    nc = tc.nc
    with ExitStack() as ctx:
        const = ctx.enter_context(tc.tile_pool(name="const", bufs=1))
        xpool = ctx.enter_context(tc.tile_pool(name="xpool", bufs=NX))
        gpool = ctx.enter_context(tc.tile_pool(name="gpool", bufs=3))
        cpool = ctx.enter_context(tc.tile_pool(name="cpool", bufs=2))
        ypool = ctx.enter_context(tc.tile_pool(name="ypool", bufs=2))
        ppool = ctx.enter_context(tc.tile_pool(name="ppool", bufs=2))
        spool = ctx.enter_context(tc.tile_pool(name="spool", bufs=2))
        jpool = ctx.enter_context(tc.tile_pool(name="jpool", bufs=1))
        small = ctx.enter_context(tc.tile_pool(name="small", bufs=4))
        stage = ctx.enter_context(tc.tile_pool(name="stage", bufs=3))
        psum_tp = ctx.enter_context(tc.psum_pool(name="psum_tp", bufs=TP_BANKS))
        psum_qk = ctx.enter_context(tc.psum_pool(name="psum_qk", bufs=2))
        psum_v = ctx.enter_context(tc.psum_pool(name="psum_v", bufs=1))
        psum_tab = ctx.enter_context(tc.psum_pool(name="psum_tab", bufs=2))
        ctx.enter_context(tc.manual_schedule())

        banks, copied = [], set()
        xts, tps, groupeds, codes = {}, {}, {}, {}
        qkbanks, vbanks, ys, tabs, prods, sums, sss, rrs, stages = {}, {}, {}, {}, {}, {}, {}, {}, {}

        def load(r, cuts=1, part=0):
            j, b = divmod(r, B)
            if part == 0:
                xt = xpool.tile([P, RT * DIM], BF16, name="xt", tag="xt")
                xts[r] = xt
            src = x[b].rearrange("(p t) k -> p (t k)", t=TPB)
            width = RT * DIM // cuts
            first = j * RT * DIM + part * width
            nc.sync.dma_start(out=xts[r][:, part * width:(part + 1) * width], in_=src[:, first:first + width])

        load(0, 4, 0)
        load(0, 4, 1)
        w_raw = const.tile([P, 8, 3 * P], BF16, name="w_raw", tag="w_raw")
        nc.sync.dma_start(
            out=w_raw[:].rearrange("p (g t) n -> p g (t n)", t=4),
            in_=qkv_w.rearrange("(g q t) n -> q g (t n)", g=2, t=4),
        )
        row = const.tile([P, BANK], BF16, name="row", tag="row")
        nc.vector.memset(row[:], 0.0)
        nc.sync.dma_start(out=row[0:1, 0:3 * P], in_=qkv_b.unsqueeze(0))
        nc.sync.dma_start(out=row[0:1, 3 * P:3 * P + D], in_=q_scale.unsqueeze(0))
        nc.sync.dma_start(out=row[0:1, 3 * P + D:BANK], in_=k_scale.unsqueeze(0))
        load(0, 4, 2)
        load(0, 4, 3)
        pe_sb = const.tile([P, TPB * P], BF16, name="pe_sb", tag="pe_sb")
        pe_src = pe[0, 0].rearrange("(p t) i a b -> p (t i a b)", t=TPB)
        nc.sync.dma_start(out=pe_sb[:, 0:4 * P], in_=pe_src[:, 0:4 * P])
        load(1)
        for r in range(2, NX):
            load(r)
        nc.sync.dma_start(out=pe_sb[:, 4 * P:], in_=pe_src[:, 4 * P:])

        ident = const.tile([P, P], F32, name="ident", tag="ident")
        make_identity(nc, ident[:])
        ones = const.tile([P, P], BF16, name="ones", tag="ones")
        nc.vector.memset(ones[:], 1.0)
        eps = const.tile([P, 1], F32, name="eps", tag="eps")
        nc.vector.memset(eps[:], EPS)
        ident_bf = const.tile([P, P], BF16, name="ident_bf", tag="ident_bf")
        nc.vector.tensor_copy(out=ident_bf[:], in_=ident[:])
        junk = const.tile([P, 1], F32, name="junk", tag="junk")
        nc.scalar.activation(out=junk[:], in_=eps[:], func=ACT.Abs_reciprocal_sqrt)

        def transposes(u):
            r, tt = divmod(u, RT)
            words = xts[r][:].bitcast(F32)
            tp = psum_tp.tile([P, 4, P], F32, name="tp", tag="tp")
            for c in range(4):
                col = tt * WORDS + (c // 2) * 2 * P + c % 2
                nc.tensor.transpose(tp[:, c, :], words[:, col:col + 2 * P - 1:2], ident[:])
            tps[u] = tp
            banks.append(u)
            if tt == RT - 1 and r + NX < ROUNDS:
                load(r + NX)

        def copy_out(u):
            r, tt = divmod(u, RT)
            if tt == 0:
                grouped = gpool.tile([P, RT * DIM], BF16, name="grouped", tag="grouped", align_bytes=64)
                groupeds[r] = grouped
            nc.scalar.copy(
                out=groupeds[r][:].bitcast(F32)[:, tt * WORDS:(tt + 1) * WORDS].rearrange("p (g r v) -> p g r v", g=2, v=2),
                in_=tps[u][:].rearrange("p (g v) r -> p g r v", v=2),
            )
            copied.add(u)

        def fill_banks(most=TP_BANKS):
            for n in range(most):
                u = len(tps)
                if u < TILES and (len(banks) < TP_BANKS or banks[-TP_BANKS] in copied):
                    transposes(u)

        def quantise(r, cuts=1):
            xc = cpool.tile([P, RT * 2 * P], U32, name="xc", tag="xc", align_bytes=64)
            xs = cpool.tile([P, RT * 2 * P], U8, name="xs", tag="xs", align_bytes=64)
            codes[r] = xc, xs
            width = RT * 2 * P // cuts

            def part(c):
                nc.vector.quantize_mx(
                    out=xc[:, c * width:(c + 1) * width].bitcast(FP8X4),
                    scales=xs[:, c * width:(c + 1) * width],
                    in_=groupeds[r][:, 4 * c * width:4 * (c + 1) * width],
                )

            return part

        def project(r, tiles, bank, width, wc, ws):
            xc, xs = codes[r]
            for n, tt in enumerate(tiles):
                for g in range(2):
                    sl = slice((tt * 2 + g) * P, (tt * 2 + g + 1) * P)
                    nc.tensor.matmul_mx(
                        out=bank[:, n * width:(n + 1) * width],
                        lhsT=xc[:, sl].bitcast(FP8X4), lhsT_scale=xs[:, sl],
                        rhs=wc[:, g * width:(g + 1) * width].bitcast(FP8X4), rhs_scale=ws[:, g * width:(g + 1) * width],
                        start=(g == 0), stop=(g == 1),
                    )

        def project_qk(r, half):
            qkb = psum_qk.tile([P, BANK], F32, name="qkb", tag="qkb")
            qkbanks[r, half] = qkb
            project(r, range(half * HALF, (half + 1) * HALF), qkb, QK, wc_qk, ws_qk)

        def project_v(r):
            vb = psum_v.tile([P, BANK], F32, name="vb", tag="vb")
            vbanks[r] = vb
            project(r, range(RT), vb, P, wc_v, ws_v)

        def stage_tile(kind, r, rows):
            if (kind, r) not in stages:
                st = stage.tile([P, rows, RT, D], F32, name=kind, tag=kind)
                stages[kind, r] = st
            return stages[kind, r]

        def store(dst, kind, r, row, first=0, last=RT):
            j, b = divmod(r, B)
            view = dst[b].rearrange("h (p t) d -> p h (t d)", t=TPB)
            nc.sync.dma_start(
                out=view[:, :, (j * RT + first) * D:(j * RT + last) * D],
                in_=stages[kind, r][:, row:row + H, first:last, :].rearrange("p h t d -> p h (t d)"),
            )

        def add_bias(r):
            y = ypool.tile([P, RT, QK], F32, name="y", tag="y")
            for half in range(2):
                nc.vector.tensor_tensor(
                    out=y[:, HALF * half:HALF * (half + 1), :],
                    in0=qkbanks[r, half][:].rearrange("p (t c) -> p t c", t=HALF),
                    in1=bias_qk[:].unsqueeze(1).to_broadcast([P, HALF, QK]),
                    op=ALU.add,
                )
            ys[r] = y
            vst = stage_tile("vst", r, H)
            nc.vector.tensor_tensor(
                out=vst[:].rearrange("p h t d -> p t h d"),
                in0=vbanks[r][:].rearrange("p (t h d) -> p t h d", t=RT, h=H),
                in1=cv[:, 0:P].rearrange("p (h d) -> p h d", h=H).unsqueeze(1).to_broadcast([P, RT, H, D]),
                op=ALU.add,
            )
            store(out_2, "vst", r, 0)

        def squares(r):
            ss = small.tile([P, GROUPS], F32, name="ss", tag="ss")
            sq = jpool.tile([P, GROUPS, D], F32, name="sq", tag="sq")
            for n in range(GROUPS):
                tt, m = divmod(n, ROWS)
                nc.scalar.activation(
                    out=sq[:, n, :], in_=ys[r][:, tt, m * D:(m + 1) * D], func=ACT.Square, accum_out=ss[:, n:n + 1],
                )
            sss[r] = ss

        def norms(r):
            rr = small.tile([P, GROUPS], F32, name="rr", tag="rr")
            nc.scalar.activation(out=rr[:], in_=sss[r][:], func=ACT.Abs_reciprocal_sqrt, scale=1.0 / D, bias=eps[:])
            rrs[r] = rr

        def table(j, half):
            tab = psum_tab.tile([P, HALF, 2 * P], F32, name="tab", tag="tab")
            for tt in range(HALF):
                nc.tensor.matmul(out=tab[:, tt, :], lhsT=pe_t[:, j * RT + half * HALF + tt, :], rhs=diag[:], start=True, stop=True)
            tabs[j, half] = tab

        def products(r, half):
            if half == 0:
                pr = ppool.tile([P, GROUPS, 2, D], F32, name="pr", tag="pr")
                prods[r] = pr
            shape = [P, HALF * 2, H, D, 2]
            nc.vector.tensor_tensor(
                out=prods[r][:, half * HALF * ROWS:(half + 1) * HALF * ROWS].rearrange("p (m h) b (i a) -> p m h (b i) a", h=H, a=2),
                in0=tabs[r // B, half][:].rearrange("p t (s c a) -> p (t s) c a", s=2, a=2).unsqueeze(2).to_broadcast(shape),
                in1=ys[r][:, half * HALF:(half + 1) * HALF, :].rearrange("p t (s h c) -> p (t s) h c", s=2, h=H).unsqueeze(4).to_broadcast(shape),
                op=ALU.mult,
            )

        def sums_tile(r):
            sm = spool.tile([P, GROUPS, D], F32, name="sm", tag="sm")
            sums[r] = sm

        def pair_add(r, first, last, eng):
            eng.tensor_tensor(
                out=sums[r][:, first:last, :], in0=prods[r][:, first:last, 0, :], in1=prods[r][:, first:last, 1, :], op=ALU.add,
            )

        def scale_by_scalar(r, count):
            st = stage_tile("qkst", r, ROWS)
            for n in range(count):
                tt, m = divmod(n, ROWS)
                nc.scalar.activation(out=st[:, m, tt, :], in_=sums[r][:, n, :], func=ACT.Copy, scale=rrs[r][:, n:n + 1])

        def scale_by_vector(r, count):
            st = stage_tile("qkst", r, ROWS)
            tiles = (GROUPS - count) // ROWS
            nc.vector.tensor_tensor(
                out=st[:, :, RT - tiles:, :].rearrange("p m t d -> p t m d"),
                in0=sums[r][:, count:, :].rearrange("p (t m) d -> p t m d", t=tiles),
                in1=rrs[r][:, count:].rearrange("p (t m) -> p t m", t=tiles).unsqueeze(3).to_broadcast([P, tiles, ROWS, D]),
                op=ALU.mult,
            )

        def store_qk(r, first=0, last=RT):
            store(out_0, "qkst", r, 0, first, last)
            store(out_1, "qkst", r, H, first, last)

        def constants():
            cps = psum_tab.tile([P, BANK], F32, name="cps", tag="tab")
            nc.tensor.matmul(out=cps[:], lhsT=ones[:], rhs=row[:], start=True, stop=True)
            nc.scalar.copy(
                out=bias_qk[:].rearrange("p (n b i) -> p n b i", b=2, i=PAIRS),
                in_=cps[:, 0:QK].rearrange("p (n i b) -> p n b i", i=PAIRS, b=2),
            )
            nc.scalar.copy(out=cv[:], in_=cps[:, QK:BANK])
            for s in range(2):
                nc.gpsimd.tensor_tensor(
                    out=diag[:, s * P:(s + 1) * P].rearrange("p (b i a) -> p b i a", b=2, a=2),
                    in0=ident[:].rearrange("p (i a b) -> p b i a", a=2, b=2),
                    in1=cv[:, P + s * D:P + (s + 1) * D].rearrange("p (i b) -> p b i", b=2).unsqueeze(3).to_broadcast([P, 2, PAIRS, 2]),
                    op=ALU.mult,
                )

        bias_qk = const.tile([P, QK], F32, name="bias_qk", tag="bias_qk")
        cv = const.tile([P, QK], F32, name="cv", tag="cv")
        diag = const.tile([P, 2 * P], BF16, name="diag", tag="diag")
        pe_t = const.tile([P, TPB, P], BF16, name="pe_t", tag="pe_t")

        def transpose_pe(j):
            tp = psum_tp.tile([P, RT, P], BF16, name="tpe", tag="tp")
            for t in range(RT):
                nc.tensor.transpose(tp[:, t, :], pe_sb[:, (RT * j + t) * P:(RT * j + t + 1) * P], ident_bf[:])
            nc.scalar.copy(out=pe_t[:, RT * j:RT * (j + 1), :], in_=tp[:])
            banks.append(("pe", j))
            copied.add(("pe", j))

        wg_qk = const.tile([P, 2, QK, 4], BF16, name="wg_qk", tag="wg_qk", align_bytes=64)
        wg_v = const.tile([P, 2, P, 4], BF16, name="wg_v", tag="wg_v", align_bytes=64)
        wc_qk = const.tile([P, 2 * QK], U32, name="wc_qk", tag="wc_qk", align_bytes=64)
        ws_qk = const.tile([P, 2 * QK], U8, name="ws_qk", tag="ws_qk", align_bytes=64)
        wc_v = const.tile([P, 2 * P], U32, name="wc_v", tag="wc_v", align_bytes=64)
        ws_v = const.tile([P, 2 * P], U8, name="ws_v", tag="ws_v", align_bytes=64)

        def weights_qk():
            for g in range(2):
                for b in range(2):
                    nc.vector.tensor_copy(
                        out=wg_qk[:, g].rearrange("p (n b i) t -> p n b i t", n=4, b=2)[:, :, b],
                        in_=w_raw[:, 4 * g:4 * g + 4, 0:QK].rearrange("p t (n i b) -> p n i t b", i=PAIRS, b=2)[:, :, :, :, b],
                    )
            nc.vector.quantize_mx(out=wc_qk[:].bitcast(FP8X4), scales=ws_qk[:], in_=wg_qk[:].rearrange("p g n t -> p (g n t)"))

        def weights_v():
            for g in range(2):
                nc.vector.tensor_copy(out=wg_v[:, g], in_=w_raw[:, 4 * g:4 * g + 4, QK:3 * P].rearrange("p t n -> p n t"))
            nc.vector.quantize_mx(out=wc_v[:].bitcast(FP8X4), scales=ws_v[:], in_=wg_v[:].rearrange("p g n t -> p (g n t)"))

        def live(r):
            return 0 <= r < ROUNDS

        fill_banks(2)
        copy_out(0)
        copy_out(1)
        constants()
        fill_banks(2)
        copy_out(2)
        copy_out(3)
        transpose_pe(0)
        weights_qk()
        quantise_part = quantise(0, 2)
        quantise_part(0)
        project_qk(0, 0)
        fill_banks(2)
        quantise_part(1)
        project_qk(0, 1)
        weights_v()
        fill_banks(1)
        project_v(0)
        for half in range(2):
            table(0, half)
        fill_banks()
        for u in range(4, 10):
            copy_out(u)
            fill_banks()
        for i in range(ROUNDS):
            u0 = 10 + i * RT
            if live(i - 2):
                scale_by_scalar(i - 2, SCALAR_GROUPS)
            for u in (u0, u0 + 1):
                if u < TILES:
                    copy_out(u)
            if i == 0:
                add_bias(0)
                products(0, 0)
                products(0, 1)
            if live(i + 1):
                quantise(i + 1)(0)
            if live(i - 1):
                sums_tile(i - 1)
                if live(i + 1):
                    nc.vector.memset(sums[i - 1][:, 0, 0:1], 0.0)
            if i > 0:
                add_bias(i)
            if live(i + 1):
                project_qk(i + 1, 0)
                project_qk(i + 1, 1)
                project_v(i + 1)
            fill_banks()
            if live(i - 1):
                pair_add(i - 1, 0, GROUPS, nc.gpsimd)
            squares(i)
            for u in (u0 + 2, u0 + 3):
                if u < TILES:
                    copy_out(u)
                if u == u0 + 2:
                    norms(i)
            for half in range(2):
                if i > 0:
                    products(i, half)
                if i % B == B - 1 and live(i + 1):
                    table((i + 1) // B, half)
            if live(i - 2):
                scale_by_vector(i - 2, SCALAR_GROUPS)
                store_qk(i - 2)
            if i + 1 < ROUNDS // B:
                transpose_pe(i + 1)
            fill_banks()
        r = ROUNDS - 1
        scale_by_scalar(r - 1, GROUPS)
        store_qk(r - 1)
        sums_tile(r)
        pair_add(r, 0, ROWS, nc.gpsimd)
        pair_add(r, ROWS, GROUPS, nc.vector)
        scale_by_vector(r, GROUPS // 2)
        store_qk(r, HALF, RT)
        scale_by_scalar(r, GROUPS // 2)
        store_qk(r, 0, HALF)
